import numpy as np
import ml_dtypes


def mxq(x, axis, fmt="e4m3"):
    dtype, down = {"e4m3": (ml_dtypes.float8_e4m3fn, 7), "e5m2": (ml_dtypes.float8_e5m2, 14)}[fmt]
    v = np.moveaxis(np.asarray(x, np.float32).astype(ml_dtypes.bfloat16).astype(np.float64), axis, -1)
    blocks = v.reshape(v.shape[:-1] + (-1, 32))
    amax = np.abs(blocks).max(-1, keepdims=True)
    byte = np.maximum(np.where(amax > 0, np.frexp(amax)[1] - 1 + 127, 0) - down, 1)
    scale = np.exp2(byte - 127.0)
    codes = (blocks / scale).astype(np.float32).astype(dtype).astype(np.float64)
    return np.moveaxis((codes * scale).reshape(v.shape), -1, axis)


WIDE = False


def mx_kscale(k):
    if not WIDE:
        return np.ones(k)
    levels = np.array([10, -10, 5, -5, 0])
    a = np.random.permutation(np.resize(levels, k // 512 * 4)).reshape(k // 512, 4)
    idx = np.arange(k)
    return np.exp2(a[idx // 512, idx % 128 // 32])


BF16 = ml_dtypes.bfloat16


def bf(x):
    return np.asarray(x, np.float32).astype(BF16)


def f64(x):
    return np.asarray(x).astype(np.float64)


B, S, D, H, E, LAYERS, PLEN = 32, 1024, 512, 8, 512, 32, 4
LQ = LAYERS * PLEN


def setup_inputs():
    s, t = mx_kscale(D), mx_kscale(D)
    common = np.random.standard_normal((1, 1, D)) * 0.2
    return {"pos_o": bf((common + np.random.standard_normal((B, LQ, D)) * 0.2) * s),
            "neg_o": bf((common + np.random.standard_normal((B, LQ, D)) * 0.07) * s),
            "Wo": bf(np.random.standard_normal((D, D)) * 2.0 / np.sqrt(D) / s[:, None] * t),
            "bo": bf(np.random.standard_normal(D) * 0.2 * t),
            "Wp": bf(np.random.standard_normal((D, E)) * 1.5 / np.sqrt(D) / t[:, None]),
            "bp": bf(np.random.standard_normal(E) * 0.2)}


def reference(pos_o, neg_o, Wo, bo, Wp, bp):
    woq = mxq(f64(Wo), 0, "e4m3")
    wpq = mxq(f64(Wp), 0, "e4m3")
    pos_h = (mxq(f64(pos_o), 2, "e4m3") @ woq) + f64(bo)
    neg_h = (mxq(f64(neg_o), 2, "e4m3") @ woq) + f64(bo)
    pos_p = (mxq(pos_h, 2, "e4m3") @ wpq) + f64(bp)
    neg_p = (mxq(neg_h, 2, "e4m3") @ wpq) + f64(bp)
    xy = np.sum(pos_p * neg_p, axis=-1, keepdims=True)
    xx = np.sum(pos_p * pos_p, axis=-1, keepdims=True)
    neg_p = neg_p - (xy / (xx + 1e-8)) * pos_p
    return pos_p.reshape(B, LAYERS, PLEN, E), neg_p.reshape(B, LAYERS, PLEN, E)

@@ -1,0 +1,244 @@
+from contextlib import ExitStack
+
+import concourse.mybir as mybir
+from concourse.masks import make_identity
+
+F32 = mybir.dt.float32
+BF16 = mybir.dt.bfloat16
+U32 = mybir.dt.uint32
+U8 = mybir.dt.uint8
+FP8X4 = mybir.dt.float8_e4m3fn_x4
+ALU = mybir.AluOpType
+ACT = mybir.ActivationFunctionType
+
+P = 128
+D = 512
+ROWS = 4096
+NT = ROWS // P
+NSTEP = NT // 2
+COLS = 512
+EPS = 1e-8
+FLOPS = 2 * 2 * (2 * ROWS) * D * D
+
+PIN = False
+REGROUP = "gpsimd"
+
+
+def tile_qkvorthoposnegpromptg_pb_t_kernel(tc, pos_o, neg_o, Wo, bo, Wp, bp, out_0, out_1):
+    nc = tc.nc
+    xs = [a.flatten_outer_dims().rearrange("(p n) k -> p n k", n=NT) for a in (pos_o, neg_o)]
+    outs = [a.flatten_outer_dims().rearrange("(p n) e -> p n e", n=NT) for a in (out_0, out_1)]
+
+    with ExitStack() as ctx:
+        const = ctx.enter_context(tc.tile_pool(name="const", bufs=1))
+        xpool = ctx.enter_context(tc.tile_pool(name="xpool", bufs=1))
+        work = ctx.enter_context(tc.tile_pool(name="work", bufs=2))
+        outp = ctx.enter_context(tc.tile_pool(name="outp", bufs=3))
+        small = ctx.enter_context(tc.tile_pool(name="small", bufs=3))
+        ps_s = ctx.enter_context(tc.psum_pool(name="ps_s", bufs=4))
+        ps_v = ctx.enter_context(tc.psum_pool(name="ps_v", bufs=2))
+        if PIN:
+            ctx.enter_context(tc.manual_schedule())
+
+        ident = const.tile([P, P], F32, name="ident")
+        make_identity(nc, ident[:])
+        bo_raw = const.tile([P, 4], BF16, name="bo_raw")
+        nc.gpsimd.dma_start(out=bo_raw[:], in_=bo.rearrange("(p t) -> p t", t=4))
+        bp_raw = const.tile([P, D], BF16, name="bp_raw")
+        nc.gpsimd.dma_start(out=bp_raw[:], in_=bp.partition_broadcast(P))
+
+        xin = {}
+
+        def load_x(j):
+            for s in range(2):
+                t = xpool.tile([P, 2, D], BF16, name="xin_%d_%d" % (s, j))
+                nc.sync.dma_start(out=t[:], in_=xs[s][:, 2 * j : 2 * j + 2, :])
+                xin[(s, j)] = t
+
+        load_x(0)
+        wo_raw = const.tile([P, 4, D], BF16, name="wo_raw")
+        for u in range(2):
+            nc.sync.dma_start(
+                out=wo_raw[:, 2 * u : 2 * u + 2, :],
+                in_=Wo[256 * u : 256 * u + 256, :].rearrange("(q e) c -> q e c", e=2),
+            )
+        load_x(1)
+        wp_raw = const.tile([P, 4, D], BF16, name="wp_raw")
+        nc.sync.dma_start(out=wp_raw[:], in_=Wp.rearrange("(p t) e -> p t e", t=4))
+        for j in range(2, NSTEP):
+            load_x(j)
+
+        wo_g = const.tile([P, 4, P, 4], BF16, name="wo_g", align_bytes=64)
+        nc.vector.tensor_copy(out=wo_g[:], in_=wo_raw[:].rearrange("q t (m b) -> q b m t", b=4))
+        wo_c = const.tile([P, D], U32, name="wo_c", align_bytes=64)
+        wo_s = const.tile([P, D], U8, name="wo_s", align_bytes=64)
+        bo_f = const.tile([P, 4], F32, name="bo_f")
+        nc.vector.tensor_copy(out=bo_f[:], in_=bo_raw[:])
+        nc.vector.quantize_mx(out=wo_c[:].bitcast(FP8X4), scales=wo_s[:], in_=wo_g[:].rearrange("q b m t -> q (b m t)"))
+
+        beta = const.tile([P, D], F32, name="beta")
+        wp_c = const.tile([P, D], U32, name="wp_c", align_bytes=64)
+        wp_s = const.tile([P, D], U8, name="wp_s", align_bytes=64)
+        wn_c = const.tile([P, D], U32, name="wn_c", align_bytes=64)
+        wn_s = const.tile([P, D], U8, name="wn_s", align_bytes=64)
+
+        def prepare_wp():
+            wp_g = const.tile([P, D, 4], BF16, name="wp_g", align_bytes=64)
+            wn_g = const.tile([P, D, 4], BF16, name="wn_g", align_bytes=64)
+            src = wp_raw[:].rearrange("p t e -> p e t")
+            nc.vector.tensor_copy(out=wp_g[:], in_=src)
+            nc.vector.tensor_scalar_mul(out=wn_g[:], in0=src, scalar1=-1.0)
+            nc.vector.tensor_copy(out=beta[:], in_=bp_raw[:])
+            nc.vector.quantize_mx(out=wp_c[:].bitcast(FP8X4), scales=wp_s[:], in_=wp_g[:].rearrange("p e t -> p (e t)"))
+            nc.vector.quantize_mx(out=wn_c[:].bitcast(FP8X4), scales=wn_s[:], in_=wn_g[:].rearrange("p e t -> p (e t)"))
+
+        st = {}
+
+        def transposes(j):
+            xg = work.tile([P, 4 * COLS], BF16, name="xg", align_bytes=64)
+            xg_w = xg[:].bitcast(F32).rearrange("p (c u) -> p c u", u=2)
+            for s in range(2):
+                xt = ps_s.tile([P, 2, 256], F32, name="xt", tag="sx")
+                for i in range(2):
+                    words = xin[(s, j)][:, i, :].bitcast(F32)
+                    for u in range(2):
+                        nc.tensor.transpose(xt[:, u, P * i : P * i + P], words[:, P * u : P * u + P], ident[:])
+                nc.scalar.copy(out=xg_w[:, 256 * s : 256 * s + 256, :], in_=xt[:].rearrange("p u c -> p c u"))
+            st[("xg", j)] = xg
+            xc = work.tile([P, COLS], U32, name="xc", align_bytes=64)
+            xsc = work.tile([P, COLS], U8, name="xsc", align_bytes=64)
+            st[("xc", j)] = (xc, xsc)
+
+        def quant_half(src, dst, h):
+            codes, scales = dst
+            nc.vector.quantize_mx(
+                out=codes[:, 256 * h : 256 * h + 256].bitcast(FP8X4),
+                scales=scales[:, 256 * h : 256 * h + 256],
+                in_=src[:, 1024 * h : 1024 * h + 1024],
+            )
+
+        def hidden(j):
+            xc, xsc = st[("xc", j)]
+            hb = work.tile([P, 4, COLS], BF16, name="hb")
+            for t in range(4):
+                hp = ps_s.tile([P, COLS], F32, name="hp", tag="sx")
+                nc.tensor.matmul_mx(
+                    out=hp[:],
+                    lhsT=wo_c[:, P * t : P * t + P].bitcast(FP8X4),
+                    lhsT_scale=wo_s[:, P * t : P * t + P],
+                    rhs=xc[:].bitcast(FP8X4),
+                    rhs_scale=xsc[:],
+                    start=True,
+                    stop=True,
+                )
+                nc.scalar.activation(out=hb[:, t, :], in_=hp[:], func=ACT.Identity, bias=bo_f[:, t : t + 1], scale=1.0)
+            hg = work.tile([P, 4 * COLS], BF16, name="hg", align_bytes=64)
+            hg3 = hg[:].rearrange("p (c t) -> p c t", t=4)
+            for h in range(2):
+                src = hb[:, :, 256 * h : 256 * h + 256].rearrange("p t c -> p c t")
+                dst = hg3[:, 256 * h : 256 * h + 256, :]
+                if REGROUP == "gpsimd":
+                    nc.gpsimd.tensor_scalar(out=dst, in0=src, scalar1=1.0, scalar2=0.0, op0=ALU.mult, op1=ALU.add)
+                else:
+                    nc.vector.tensor_copy(out=dst, in_=src)
+            st[("hg", j)] = hg
+            hc = work.tile([P, COLS], U32, name="hc", align_bytes=64)
+            hs = work.tile([P, COLS], U8, name="hs", align_bytes=64)
+            st[("hc", j)] = (hc, hs)
+
+        def mx2(out, j, m, w_c, w_s, start, stop):
+            hc, hs = st[("hc", j)]
+            nc.tensor.matmul_mx(
+                out=out,
+                lhsT=hc[:, P * m : P * m + P].bitcast(FP8X4),
+                lhsT_scale=hs[:, P * m : P * m + P],
+                rhs=w_c[:].bitcast(FP8X4),
+                rhs_scale=w_s[:],
+                start=start,
+                stop=stop,
+            )
+
+        def second_pos(j):
+            tiles = []
+            for i in range(2):
+                a = ps_v.tile([P, D], F32, name="a")
+                mx2(a[:], j, i, wp_c, wp_s, True, True)
+                tiles.append(a)
+            st[("a", j)] = tiles
+
+        def second_diff(j):
+            tiles = []
+            for i in range(2):
+                d = ps_v.tile([P, D], F32, name="d")
+                mx2(d[:], j, 2 + i, wp_c, wp_s, True, False)
+                mx2(d[:], j, i, wn_c, wn_s, False, True)
+                tiles.append(d)
+            st[("d", j)] = tiles
+
+        def sums(j):
+            a, d = st[("a", j)], st[("d", j)]
+            po = outp.tile([P, 2, D], F32, name="po")
+            xx = small.tile([P, 2], F32, name="xx")
+            ss = small.tile([P, 2], F32, name="ss")
+            for i in range(2):
+                nc.vector.tensor_tensor(out=po[:, i, :], in0=a[i][:], in1=beta[:], op=ALU.add)
+            for i in range(2):
+                sq = work.tile([P, D], BF16, name="sq")
+                nc.scalar.activation(out=sq[:], in_=po[:, i, :], func=ACT.Square, accum_out=xx[:, i : i + 1])
+            nc.sync.dma_start(out=outs[0][:, 2 * j : 2 * j + 2, :], in_=po[:])
+            for i in range(2):
+                pr = work.tile([P, D], BF16, name="pr")
+                nc.vector.scalar_tensor_tensor(
+                    out=pr[:], in0=d[i][:], scalar=1.0, in1=po[:, i, :], op0=ALU.mult, op1=ALU.mult,
+                    accum_out=ss[:, i : i + 1],
+                )
+            st[("e", j)] = (po, xx, ss)
+
+        def project(j):
+            po, xx, ss = st[("e", j)]
+            g = st[("g", j)]
+            d = st[("d", j)]
+            ng = outp.tile([P, 2, D], F32, name="ng")
+            for i in range(2):
+                nc.vector.scalar_tensor_tensor(
+                    out=ng[:, i, :], in0=po[:, i, :], scalar=g[:, i : i + 1], in1=d[i][:], op0=ALU.mult, op1=ALU.add
+                )
+            nc.sync.dma_start(out=outs[1][:, 2 * j : 2 * j + 2, :], in_=ng[:])
+
+        def ok(j):
+            return 0 <= j < NSTEP
+
+        for j in range(-4, NSTEP):
+            if ok(j):
+                sums(j)
+            if ok(j + 2):
+                hidden(j + 2)
+            if ok(j + 3):
+                quant_half(st[("xg", j + 3)], st[("xc", j + 3)], 0)
+            if ok(j):
+                po, xx, ss = st[("e", j)]
+                nden = small.tile([P, 2], F32, name="nden")
+                nc.vector.tensor_scalar(out=nden[:], in0=xx[:], scalar1=-1.0, scalar2=EPS, op0=ALU.mult, op1=ALU.subtract)
+            if ok(j + 3):
+                quant_half(st[("xg", j + 3)], st[("xc", j + 3)], 1)
+            if j == -3:
+                prepare_wp()
+            if ok(j):
+                nrec = small.tile([P, 2], F32, name="nrec")
+                nc.vector.reciprocal(out=nrec[:], in_=nden[:])
+            if ok(j + 1):
+                quant_half(st[("hg", j + 1)], st[("hc", j + 1)], 0)
+            if ok(j):
+                g = small.tile([P, 2], F32, name="g")
+                nc.vector.scalar_tensor_tensor(out=g[:], in0=ss[:], scalar=EPS, in1=nrec[:], op0=ALU.subtract, op1=ALU.mult)
+                st[("g", j)] = g
+            if ok(j + 1):
+                quant_half(st[("hg", j + 1)], st[("hc", j + 1)], 1)
+            if ok(j + 4):
+                transposes(j + 4)
+            if ok(j + 1):
+                second_pos(j + 1)
+            if ok(j):
+                project(j)
+            if ok(j + 1):
+                second_diff(j + 1)

@@ -20,7 +20,7 @@ COLS = 512
 EPS = 1e-8
 FLOPS = 2 * 2 * (2 * ROWS) * D * D
 
-PIN = False
+PIN = True
 REGROUP = "gpsimd"
 
 

@@ -15,19 +15,24 @@ P = 128
 D = 512
 ROWS = 4096
 NT = ROWS // P
-NSTEP = NT // 2
-COLS = 512
 EPS = 1e-8
 FLOPS = 2 * 2 * (2 * ROWS) * D * D
 
 PIN = True
-REGROUP = "gpsimd"
+SIZES = [2] * 16
+NDEN_ON_SCALAR = True
+WP_ON_GPSIMD = False
+WP_AT = -2
+HG_BUFS = 1
+assert sum(SIZES) == NT
 
 
 def tile_qkvorthoposnegpromptg_pb_t_kernel(tc, pos_o, neg_o, Wo, bo, Wp, bp, out_0, out_1):
     nc = tc.nc
     xs = [a.flatten_outer_dims().rearrange("(p n) k -> p n k", n=NT) for a in (pos_o, neg_o)]
     outs = [a.flatten_outer_dims().rearrange("(p n) e -> p n e", n=NT) for a in (out_0, out_1)]
+    nstep = len(SIZES)
+    first = [sum(SIZES[:j]) for j in range(nstep)]
 
     with ExitStack() as ctx:
         const = ctx.enter_context(tc.tile_pool(name="const", bufs=1))
@@ -51,77 +56,97 @@ def tile_qkvorthoposnegpromptg_pb_t_kernel(tc, pos_o, neg_o, Wo, bo, Wp, bp, out
 
         def load_x(j):
             for s in range(2):
-                t = xpool.tile([P, 2, D], BF16, name="xin_%d_%d" % (s, j))
-                nc.sync.dma_start(out=t[:], in_=xs[s][:, 2 * j : 2 * j + 2, :])
+                t = xpool.tile([P, SIZES[j], D], BF16, name="xin_%d_%d" % (s, j))
+                nc.sync.dma_start(out=t[:], in_=xs[s][:, first[j] : first[j] + SIZES[j], :])
                 xin[(s, j)] = t
 
-        load_x(0)
         wo_raw = const.tile([P, 4, D], BF16, name="wo_raw")
         for u in range(2):
             nc.sync.dma_start(
                 out=wo_raw[:, 2 * u : 2 * u + 2, :],
                 in_=Wo[256 * u : 256 * u + 256, :].rearrange("(q e) c -> q e c", e=2),
             )
+        load_x(0)
         load_x(1)
         wp_raw = const.tile([P, 4, D], BF16, name="wp_raw")
         nc.sync.dma_start(out=wp_raw[:], in_=Wp.rearrange("(p t) e -> p t e", t=4))
-        for j in range(2, NSTEP):
+        for j in range(2, nstep):
             load_x(j)
 
         wo_g = const.tile([P, 4, P, 4], BF16, name="wo_g", align_bytes=64)
-        nc.vector.tensor_copy(out=wo_g[:], in_=wo_raw[:].rearrange("q t (m b) -> q b m t", b=4))
         wo_c = const.tile([P, D], U32, name="wo_c", align_bytes=64)
         wo_s = const.tile([P, D], U8, name="wo_s", align_bytes=64)
         bo_f = const.tile([P, 4], F32, name="bo_f")
-        nc.vector.tensor_copy(out=bo_f[:], in_=bo_raw[:])
-        nc.vector.quantize_mx(out=wo_c[:].bitcast(FP8X4), scales=wo_s[:], in_=wo_g[:].rearrange("q b m t -> q (b m t)"))
+
+        def prepare_wo():
+            nc.vector.tensor_copy(out=wo_g[:], in_=wo_raw[:].rearrange("q t (m b) -> q b m t", b=4))
+            nc.vector.tensor_copy(out=bo_f[:], in_=bo_raw[:])
+            nc.vector.quantize_mx(out=wo_c[:].bitcast(FP8X4), scales=wo_s[:], in_=wo_g[:].rearrange("q b m t -> q (b m t)"))
 
         beta = const.tile([P, D], F32, name="beta")
         wp_c = const.tile([P, D], U32, name="wp_c", align_bytes=64)
         wp_s = const.tile([P, D], U8, name="wp_s", align_bytes=64)
         wn_c = const.tile([P, D], U32, name="wn_c", align_bytes=64)
         wn_s = const.tile([P, D], U8, name="wn_s", align_bytes=64)
+        wp_g = const.tile([P, D, 4], BF16, name="wp_g", align_bytes=64)
+        wn_g = const.tile([P, D, 4], BF16, name="wn_g", align_bytes=64)
 
-        def prepare_wp():
-            wp_g = const.tile([P, D, 4], BF16, name="wp_g", align_bytes=64)
-            wn_g = const.tile([P, D, 4], BF16, name="wn_g", align_bytes=64)
+        def regroup_wp():
             src = wp_raw[:].rearrange("p t e -> p e t")
-            nc.vector.tensor_copy(out=wp_g[:], in_=src)
-            nc.vector.tensor_scalar_mul(out=wn_g[:], in0=src, scalar1=-1.0)
-            nc.vector.tensor_copy(out=beta[:], in_=bp_raw[:])
+            if WP_ON_GPSIMD:
+                for h in range(2):
+                    nc.gpsimd.tensor_scalar(
+                        out=wp_g[:, 256 * h : 256 * h + 256, :], in0=src[:, 256 * h : 256 * h + 256, :],
+                        scalar1=1.0, scalar2=0.0, op0=ALU.mult, op1=ALU.add,
+                    )
+            else:
+                nc.vector.tensor_copy(out=wp_g[:], in_=src)
+
+        def quantise_wp():
+            nc.vector.tensor_scalar_mul(out=wn_g[:], in0=wp_g[:], scalar1=-1.0)
             nc.vector.quantize_mx(out=wp_c[:].bitcast(FP8X4), scales=wp_s[:], in_=wp_g[:].rearrange("p e t -> p (e t)"))
+            nc.vector.tensor_copy(out=beta[:], in_=bp_raw[:])
             nc.vector.quantize_mx(out=wn_c[:].bitcast(FP8X4), scales=wn_s[:], in_=wn_g[:].rearrange("p e t -> p (e t)"))
 
         st = {}
 
         def transposes(j):
-            xg = work.tile([P, 4 * COLS], BF16, name="xg", align_bytes=64)
+            n = SIZES[j]
+            cols = 2 * n * P
+            xg = work.tile([P, 4 * cols], BF16, name="xg", align_bytes=64)
             xg_w = xg[:].bitcast(F32).rearrange("p (c u) -> p c u", u=2)
-            for s in range(2):
+            tiles = [(s, i) for s in range(2) for i in range(n)]
+            for b in range(cols // 256):
                 xt = ps_s.tile([P, 2, 256], F32, name="xt", tag="sx")
-                for i in range(2):
+                for v in range(2):
+                    s, i = tiles[2 * b + v]
                     words = xin[(s, j)][:, i, :].bitcast(F32)
                     for u in range(2):
-                        nc.tensor.transpose(xt[:, u, P * i : P * i + P], words[:, P * u : P * u + P], ident[:])
-                nc.scalar.copy(out=xg_w[:, 256 * s : 256 * s + 256, :], in_=xt[:].rearrange("p u c -> p c u"))
+                        nc.tensor.transpose(xt[:, u, P * v : P * v + P], words[:, P * u : P * u + P], ident[:])
+                nc.scalar.copy(out=xg_w[:, 256 * b : 256 * b + 256, :], in_=xt[:].rearrange("p u c -> p c u"))
             st[("xg", j)] = xg
-            xc = work.tile([P, COLS], U32, name="xc", align_bytes=64)
-            xsc = work.tile([P, COLS], U8, name="xsc", align_bytes=64)
+            xc = work.tile([P, cols], U32, name="xc", align_bytes=64)
+            xsc = work.tile([P, cols], U8, name="xsc", align_bytes=64)
             st[("xc", j)] = (xc, xsc)
 
-        def quant_half(src, dst, h):
-            codes, scales = dst
+        def quant_half(j, src, dst, h):
+            w = SIZES[j] * P
+            codes, scales = st[(dst, j)]
             nc.vector.quantize_mx(
-                out=codes[:, 256 * h : 256 * h + 256].bitcast(FP8X4),
-                scales=scales[:, 256 * h : 256 * h + 256],
-                in_=src[:, 1024 * h : 1024 * h + 1024],
+                out=codes[:, w * h : w * h + w].bitcast(FP8X4),
+                scales=scales[:, w * h : w * h + w],
+                in_=st[(src, j)][:, 4 * w * h : 4 * w * h + 4 * w],
             )
 
-        def hidden(j):
+        def hidden(j, blocks):
+            cols = 2 * SIZES[j] * P
             xc, xsc = st[("xc", j)]
-            hb = work.tile([P, 4, COLS], BF16, name="hb")
-            for t in range(4):
-                hp = ps_s.tile([P, COLS], F32, name="hp", tag="sx")
+            if blocks[0] == 0:
+                hb_new = work.tile([P, 4, cols], BF16, name="hb")
+                st[("hb", j)] = hb_new
+            hb = st[("hb", j)]
+            for t in blocks:
+                hp = ps_s.tile([P, cols], F32, name="hp", tag="sx")
                 nc.tensor.matmul_mx(
                     out=hp[:],
                     lhsT=wo_c[:, P * t : P * t + P].bitcast(FP8X4),
@@ -132,18 +157,18 @@ def tile_qkvorthoposnegpromptg_pb_t_kernel(tc, pos_o, neg_o, Wo, bo, Wp, bp, out
                     stop=True,
                 )
                 nc.scalar.activation(out=hb[:, t, :], in_=hp[:], func=ACT.Identity, bias=bo_f[:, t : t + 1], scale=1.0)
-            hg = work.tile([P, 4 * COLS], BF16, name="hg", align_bytes=64)
+
+        def regroup(j):
+            w = SIZES[j] * P
+            hb = st[("hb", j)]
+            hg = work.tile([P, 8 * w], BF16, name="hg", align_bytes=64, bufs=HG_BUFS)
             hg3 = hg[:].rearrange("p (c t) -> p c t", t=4)
-            for h in range(2):
-                src = hb[:, :, 256 * h : 256 * h + 256].rearrange("p t c -> p c t")
-                dst = hg3[:, 256 * h : 256 * h + 256, :]
-                if REGROUP == "gpsimd":
-                    nc.gpsimd.tensor_scalar(out=dst, in0=src, scalar1=1.0, scalar2=0.0, op0=ALU.mult, op1=ALU.add)
-                else:
-                    nc.vector.tensor_copy(out=dst, in_=src)
+            nc.gpsimd.tensor_scalar(
+                out=hg3, in0=hb[:].rearrange("p t c -> p c t"), scalar1=1.0, scalar2=0.0, op0=ALU.mult, op1=ALU.add
+            )
             st[("hg", j)] = hg
-            hc = work.tile([P, COLS], U32, name="hc", align_bytes=64)
-            hs = work.tile([P, COLS], U8, name="hs", align_bytes=64)
+            hc = work.tile([P, 2 * w], U32, name="hc", align_bytes=64)
+            hs = work.tile([P, 2 * w], U8, name="hs", align_bytes=64)
             st[("hc", j)] = (hc, hs)
 
         def mx2(out, j, m, w_c, w_s, start, stop):
@@ -160,7 +185,7 @@ def tile_qkvorthoposnegpromptg_pb_t_kernel(tc, pos_o, neg_o, Wo, bo, Wp, bp, out
 
         def second_pos(j):
             tiles = []
-            for i in range(2):
+            for i in range(SIZES[j]):
                 a = ps_v.tile([P, D], F32, name="a")
                 mx2(a[:], j, i, wp_c, wp_s, True, True)
                 tiles.append(a)
@@ -168,76 +193,83 @@ def tile_qkvorthoposnegpromptg_pb_t_kernel(tc, pos_o, neg_o, Wo, bo, Wp, bp, out
 
         def second_diff(j):
             tiles = []
-            for i in range(2):
+            for i in range(SIZES[j]):
                 d = ps_v.tile([P, D], F32, name="d")
-                mx2(d[:], j, 2 + i, wp_c, wp_s, True, False)
+                mx2(d[:], j, SIZES[j] + i, wp_c, wp_s, True, False)
                 mx2(d[:], j, i, wn_c, wn_s, False, True)
                 tiles.append(d)
             st[("d", j)] = tiles
 
         def sums(j):
+            n = SIZES[j]
             a, d = st[("a", j)], st[("d", j)]
-            po = outp.tile([P, 2, D], F32, name="po")
-            xx = small.tile([P, 2], F32, name="xx")
-            ss = small.tile([P, 2], F32, name="ss")
-            for i in range(2):
+            po = outp.tile([P, n, D], F32, name="po")
+            xx = small.tile([P, n], F32, name="xx")
+            ss = small.tile([P, n], F32, name="ss")
+            nden = small.tile([P, n], F32, name="nden")
+            for i in range(n):
                 nc.vector.tensor_tensor(out=po[:, i, :], in0=a[i][:], in1=beta[:], op=ALU.add)
-            for i in range(2):
+            for i in range(n):
                 sq = work.tile([P, D], BF16, name="sq")
                 nc.scalar.activation(out=sq[:], in_=po[:, i, :], func=ACT.Square, accum_out=xx[:, i : i + 1])
-            nc.sync.dma_start(out=outs[0][:, 2 * j : 2 * j + 2, :], in_=po[:])
-            for i in range(2):
+            if NDEN_ON_SCALAR:
+                nc.scalar.activation(out=nden[:], in_=xx[:], func=ACT.Copy, bias=-EPS, scale=-1.0)
+            nc.sync.dma_start(out=outs[0][:, first[j] : first[j] + n, :], in_=po[:])
+            for i in range(n):
                 pr = work.tile([P, D], BF16, name="pr")
                 nc.vector.scalar_tensor_tensor(
                     out=pr[:], in0=d[i][:], scalar=1.0, in1=po[:, i, :], op0=ALU.mult, op1=ALU.mult,
                     accum_out=ss[:, i : i + 1],
                 )
-            st[("e", j)] = (po, xx, ss)
+            st[("e", j)] = (po, xx, ss, nden)
 
         def project(j):
-            po, xx, ss = st[("e", j)]
+            n = SIZES[j]
+            po = st[("e", j)][0]
             g = st[("g", j)]
             d = st[("d", j)]
-            ng = outp.tile([P, 2, D], F32, name="ng")
-            for i in range(2):
+            ng = outp.tile([P, n, D], F32, name="ng")
+            for i in range(n):
                 nc.vector.scalar_tensor_tensor(
                     out=ng[:, i, :], in0=po[:, i, :], scalar=g[:, i : i + 1], in1=d[i][:], op0=ALU.mult, op1=ALU.add
                 )
-            nc.sync.dma_start(out=outs[1][:, 2 * j : 2 * j + 2, :], in_=ng[:])
+            nc.sync.dma_start(out=outs[1][:, first[j] : first[j] + n, :], in_=ng[:])
 
         def ok(j):
-            return 0 <= j < NSTEP
+            return 0 <= j < nstep
 
-        for j in range(-4, NSTEP):
+        prepare_wo()
+        for j in range(-4, nstep):
             if ok(j):
                 sums(j)
             if ok(j + 2):
-                hidden(j + 2)
-            if ok(j + 3):
-                quant_half(st[("xg", j + 3)], st[("xc", j + 3)], 0)
+                hidden(j + 2, (2, 3))
             if ok(j):
-                po, xx, ss = st[("e", j)]
-                nden = small.tile([P, 2], F32, name="nden")
-                nc.vector.tensor_scalar(out=nden[:], in0=xx[:], scalar1=-1.0, scalar2=EPS, op0=ALU.mult, op1=ALU.subtract)
-            if ok(j + 3):
-                quant_half(st[("xg", j + 3)], st[("xc", j + 3)], 1)
-            if j == -3:
-                prepare_wp()
-            if ok(j):
-                nrec = small.tile([P, 2], F32, name="nrec")
+                po, xx, ss, nden = st[("e", j)]
+                nrec = small.tile([P, SIZES[j]], F32, name="nrec")
                 nc.vector.reciprocal(out=nrec[:], in_=nden[:])
             if ok(j + 1):
-                quant_half(st[("hg", j + 1)], st[("hc", j + 1)], 0)
+                quant_half(j + 1, "hg", "hc", 0)
+            if ok(j + 3):
+                quant_half(j + 3, "xg", "xc", 0)
+                quant_half(j + 3, "xg", "xc", 1)
             if ok(j):
-                g = small.tile([P, 2], F32, name="g")
+                g = small.tile([P, SIZES[j]], F32, name="g")
                 nc.vector.scalar_tensor_tensor(out=g[:], in0=ss[:], scalar=EPS, in1=nrec[:], op0=ALU.subtract, op1=ALU.mult)
                 st[("g", j)] = g
             if ok(j + 1):
-                quant_half(st[("hg", j + 1)], st[("hc", j + 1)], 1)
+                quant_half(j + 1, "hg", "hc", 1)
+            if ok(j + 2):
+                regroup(j + 2)
+            if j == WP_AT:
+                regroup_wp()
+                quantise_wp()
             if ok(j + 4):
                 transposes(j + 4)
             if ok(j + 1):
                 second_pos(j + 1)
+            if ok(j + 3):
+                hidden(j + 3, (0, 1))
             if ok(j):
                 project(j)
             if ok(j + 1):

@@ -24,6 +24,10 @@ NDEN_ON_SCALAR = True
 WP_ON_GPSIMD = False
 WP_AT = -2
 HG_BUFS = 1
+D_BUFS = 2
+RING = 4
+HEAD_V_R = False
+BP_AFTER = 3
 assert sum(SIZES) == NT
 
 
@@ -40,7 +44,7 @@ def tile_qkvorthoposnegpromptg_pb_t_kernel(tc, pos_o, neg_o, Wo, bo, Wp, bp, out
         work = ctx.enter_context(tc.tile_pool(name="work", bufs=2))
         outp = ctx.enter_context(tc.tile_pool(name="outp", bufs=3))
         small = ctx.enter_context(tc.tile_pool(name="small", bufs=3))
-        ps_s = ctx.enter_context(tc.psum_pool(name="ps_s", bufs=4))
+        ps_s = ctx.enter_context(tc.psum_pool(name="ps_s", bufs=RING))
         ps_v = ctx.enter_context(tc.psum_pool(name="ps_v", bufs=2))
         if PIN:
             ctx.enter_context(tc.manual_schedule())
@@ -48,9 +52,8 @@ def tile_qkvorthoposnegpromptg_pb_t_kernel(tc, pos_o, neg_o, Wo, bo, Wp, bp, out
         ident = const.tile([P, P], F32, name="ident")
         make_identity(nc, ident[:])
         bo_raw = const.tile([P, 4], BF16, name="bo_raw")
-        nc.gpsimd.dma_start(out=bo_raw[:], in_=bo.rearrange("(p t) -> p t", t=4))
+        nc.sync.dma_start(out=bo_raw[:], in_=bo.rearrange("(p t) -> p t", t=4))
         bp_raw = const.tile([P, D], BF16, name="bp_raw")
-        nc.gpsimd.dma_start(out=bp_raw[:], in_=bp.partition_broadcast(P))
 
         xin = {}
 
@@ -72,6 +75,8 @@ def tile_qkvorthoposnegpromptg_pb_t_kernel(tc, pos_o, neg_o, Wo, bo, Wp, bp, out
         nc.sync.dma_start(out=wp_raw[:], in_=Wp.rearrange("(p t) e -> p t e", t=4))
         for j in range(2, nstep):
             load_x(j)
+            if j == BP_AFTER:
+                nc.sync.dma_start(out=bp_raw[:], in_=bp.partition_broadcast(P))
 
         wo_g = const.tile([P, 4, P, 4], BF16, name="wo_g", align_bytes=64)
         wo_c = const.tile([P, D], U32, name="wo_c", align_bytes=64)
@@ -100,12 +105,13 @@ def tile_qkvorthoposnegpromptg_pb_t_kernel(tc, pos_o, neg_o, Wo, bo, Wp, bp, out
                         scalar1=1.0, scalar2=0.0, op0=ALU.mult, op1=ALU.add,
                     )
             else:
-                nc.vector.tensor_copy(out=wp_g[:], in_=src)
+                nc.vector.tensor_copy(
+                    out=wp_g[:].rearrange("p (c i) t -> p c t i", i=4), in_=wp_raw[:].rearrange("p t (c i) -> p c t i", i=4)
+                )
 
         def quantise_wp():
             nc.vector.tensor_scalar_mul(out=wn_g[:], in0=wp_g[:], scalar1=-1.0)
             nc.vector.quantize_mx(out=wp_c[:].bitcast(FP8X4), scales=wp_s[:], in_=wp_g[:].rearrange("p e t -> p (e t)"))
-            nc.vector.tensor_copy(out=beta[:], in_=bp_raw[:])
             nc.vector.quantize_mx(out=wn_c[:].bitcast(FP8X4), scales=wn_s[:], in_=wn_g[:].rearrange("p e t -> p (e t)"))
 
         st = {}
@@ -163,9 +169,14 @@ def tile_qkvorthoposnegpromptg_pb_t_kernel(tc, pos_o, neg_o, Wo, bo, Wp, bp, out
             hb = st[("hb", j)]
             hg = work.tile([P, 8 * w], BF16, name="hg", align_bytes=64, bufs=HG_BUFS)
             hg3 = hg[:].rearrange("p (c t) -> p c t", t=4)
-            nc.gpsimd.tensor_scalar(
-                out=hg3, in0=hb[:].rearrange("p t c -> p c t"), scalar1=1.0, scalar2=0.0, op0=ALU.mult, op1=ALU.add
-            )
+            if HEAD_V_R and j == 0:
+                nc.vector.tensor_copy(
+                    out=hg[:].rearrange("p (c i t) -> p c t i", i=4, t=4), in_=hb[:].rearrange("p t (c i) -> p c t i", i=4)
+                )
+            else:
+                nc.gpsimd.tensor_scalar(
+                    out=hg3, in0=hb[:].rearrange("p t c -> p c t"), scalar1=1.0, scalar2=0.0, op0=ALU.mult, op1=ALU.add
+                )
             st[("hg", j)] = hg
             hc = work.tile([P, 2 * w], U32, name="hc", align_bytes=64)
             hs = work.tile([P, 2 * w], U8, name="hs", align_bytes=64)
@@ -191,18 +202,16 @@ def tile_qkvorthoposnegpromptg_pb_t_kernel(tc, pos_o, neg_o, Wo, bo, Wp, bp, out
                 tiles.append(a)
             st[("a", j)] = tiles
 
-        def second_diff(j):
-            tiles = []
-            for i in range(SIZES[j]):
-                d = ps_v.tile([P, D], F32, name="d")
-                mx2(d[:], j, SIZES[j] + i, wp_c, wp_s, True, False)
-                mx2(d[:], j, i, wn_c, wn_s, False, True)
-                tiles.append(d)
-            st[("d", j)] = tiles
+        def second_diff(j, i):
+            d = ps_v.tile([P, D], F32, name="d", bufs=D_BUFS)
+            mx2(d[:], j, SIZES[j] + i, wp_c, wp_s, True, False)
+            mx2(d[:], j, i, wn_c, wn_s, False, True)
+            st[("d", j, i)] = d
 
         def sums(j):
             n = SIZES[j]
-            a, d = st[("a", j)], st[("d", j)]
+            a = st[("a", j)]
+            d = [st[("d", j, i)] for i in range(n)]
             po = outp.tile([P, n, D], F32, name="po")
             xx = small.tile([P, n], F32, name="xx")
             ss = small.tile([P, n], F32, name="ss")
@@ -227,13 +236,16 @@ def tile_qkvorthoposnegpromptg_pb_t_kernel(tc, pos_o, neg_o, Wo, bo, Wp, bp, out
             n = SIZES[j]
             po = st[("e", j)][0]
             g = st[("g", j)]
-            d = st[("d", j)]
+            d = [st[("d", j, i)] for i in range(n)]
             ng = outp.tile([P, n, D], F32, name="ng")
             for i in range(n):
                 nc.vector.scalar_tensor_tensor(
                     out=ng[:, i, :], in0=po[:, i, :], scalar=g[:, i : i + 1], in1=d[i][:], op0=ALU.mult, op1=ALU.add
                 )
-            nc.sync.dma_start(out=outs[1][:, first[j] : first[j] + n, :], in_=ng[:])
+                if j == nstep - 1:
+                    nc.sync.dma_start(out=outs[1][:, first[j] + i : first[j] + i + 1, :], in_=ng[:, i : i + 1, :])
+            if j < nstep - 1:
+                nc.sync.dma_start(out=outs[1][:, first[j] : first[j] + n, :], in_=ng[:])
 
         def ok(j):
             return 0 <= j < nstep
@@ -261,6 +273,8 @@ def tile_qkvorthoposnegpromptg_pb_t_kernel(tc, pos_o, neg_o, Wo, bo, Wp, bp, out
                 quant_half(j + 1, "hg", "hc", 1)
             if ok(j + 2):
                 regroup(j + 2)
+            if j == -1:
+                nc.vector.tensor_copy(out=beta[:], in_=bp_raw[:])
             if j == WP_AT:
                 regroup_wp()
                 quantise_wp()
@@ -268,9 +282,13 @@ def tile_qkvorthoposnegpromptg_pb_t_kernel(tc, pos_o, neg_o, Wo, bo, Wp, bp, out
                 transposes(j + 4)
             if ok(j + 1):
                 second_pos(j + 1)
+                if D_BUFS == 3:
+                    second_diff(j + 1, 0)
             if ok(j + 3):
                 hidden(j + 3, (0, 1))
             if ok(j):
                 project(j)
             if ok(j + 1):
-                second_diff(j + 1)
+                if D_BUFS == 2:
+                    second_diff(j + 1, 0)
+                second_diff(j + 1, 1)

@@ -15,28 +15,20 @@ P = 128
 D = 512
 ROWS = 4096
 NT = ROWS // P
+N = 2
+NSTEP = NT // N
+COLS = 2 * N * P
 EPS = 1e-8
+ROOT_EPS = 1e-4
+PITCH = D + 16
+PO_BUFS = 3
 FLOPS = 2 * 2 * (2 * ROWS) * D * D
-
-PIN = True
-SIZES = [2] * 16
-NDEN_ON_SCALAR = True
-WP_ON_GPSIMD = False
-WP_AT = -2
-HG_BUFS = 1
-D_BUFS = 2
-RING = 4
-HEAD_V_R = False
-BP_AFTER = 3
-assert sum(SIZES) == NT
 
 
 def tile_qkvorthoposnegpromptg_pb_t_kernel(tc, pos_o, neg_o, Wo, bo, Wp, bp, out_0, out_1):
     nc = tc.nc
     xs = [a.flatten_outer_dims().rearrange("(p n) k -> p n k", n=NT) for a in (pos_o, neg_o)]
     outs = [a.flatten_outer_dims().rearrange("(p n) e -> p n e", n=NT) for a in (out_0, out_1)]
-    nstep = len(SIZES)
-    first = [sum(SIZES[:j]) for j in range(nstep)]
 
     with ExitStack() as ctx:
         const = ctx.enter_context(tc.tile_pool(name="const", bufs=1))
@@ -44,23 +36,27 @@ def tile_qkvorthoposnegpromptg_pb_t_kernel(tc, pos_o, neg_o, Wo, bo, Wp, bp, out
         work = ctx.enter_context(tc.tile_pool(name="work", bufs=2))
         outp = ctx.enter_context(tc.tile_pool(name="outp", bufs=3))
         small = ctx.enter_context(tc.tile_pool(name="small", bufs=3))
-        ps_s = ctx.enter_context(tc.psum_pool(name="ps_s", bufs=RING))
+        ps_s = ctx.enter_context(tc.psum_pool(name="ps_s", bufs=4))
         ps_v = ctx.enter_context(tc.psum_pool(name="ps_v", bufs=2))
-        if PIN:
-            ctx.enter_context(tc.manual_schedule())
+        ctx.enter_context(tc.manual_schedule())
 
         ident = const.tile([P, P], F32, name="ident")
         make_identity(nc, ident[:])
         bo_raw = const.tile([P, 4], BF16, name="bo_raw")
         nc.sync.dma_start(out=bo_raw[:], in_=bo.rearrange("(p t) -> p t", t=4))
         bp_raw = const.tile([P, D], BF16, name="bp_raw")
+        pos = []
+        for i in range(PO_BUFS):
+            t = const.tile([P, N, PITCH], F32, name="po_%d" % i)
+            nc.gpsimd.memset(t[:, :, D : D + 1], ROOT_EPS)
+            pos.append(t)
 
         xin = {}
 
         def load_x(j):
             for s in range(2):
-                t = xpool.tile([P, SIZES[j], D], BF16, name="xin_%d_%d" % (s, j))
-                nc.sync.dma_start(out=t[:], in_=xs[s][:, first[j] : first[j] + SIZES[j], :])
+                t = xpool.tile([P, N, D], BF16, name="xin_%d_%d" % (s, j))
+                nc.sync.dma_start(out=t[:], in_=xs[s][:, N * j : N * j + N, :])
                 xin[(s, j)] = t
 
         wo_raw = const.tile([P, 4, D], BF16, name="wo_raw")
@@ -73,22 +69,19 @@ def tile_qkvorthoposnegpromptg_pb_t_kernel(tc, pos_o, neg_o, Wo, bo, Wp, bp, out
         load_x(1)
         wp_raw = const.tile([P, 4, D], BF16, name="wp_raw")
         nc.sync.dma_start(out=wp_raw[:], in_=Wp.rearrange("(p t) e -> p t e", t=4))
-        for j in range(2, nstep):
+        for j in range(2, NSTEP):
             load_x(j)
-            if j == BP_AFTER:
+            if j == 3:
                 nc.sync.dma_start(out=bp_raw[:], in_=bp.partition_broadcast(P))
 
         wo_g = const.tile([P, 4, P, 4], BF16, name="wo_g", align_bytes=64)
         wo_c = const.tile([P, D], U32, name="wo_c", align_bytes=64)
         wo_s = const.tile([P, D], U8, name="wo_s", align_bytes=64)
-        bo_f = const.tile([P, 4], F32, name="bo_f")
 
         def prepare_wo():
             nc.vector.tensor_copy(out=wo_g[:], in_=wo_raw[:].rearrange("q t (m b) -> q b m t", b=4))
-            nc.vector.tensor_copy(out=bo_f[:], in_=bo_raw[:])
             nc.vector.quantize_mx(out=wo_c[:].bitcast(FP8X4), scales=wo_s[:], in_=wo_g[:].rearrange("q b m t -> q (b m t)"))
 
-        beta = const.tile([P, D], F32, name="beta")
         wp_c = const.tile([P, D], U32, name="wp_c", align_bytes=64)
         wp_s = const.tile([P, D], U8, name="wp_s", align_bytes=64)
         wn_c = const.tile([P, D], U32, name="wn_c", align_bytes=64)
@@ -96,20 +89,10 @@ def tile_qkvorthoposnegpromptg_pb_t_kernel(tc, pos_o, neg_o, Wo, bo, Wp, bp, out
         wp_g = const.tile([P, D, 4], BF16, name="wp_g", align_bytes=64)
         wn_g = const.tile([P, D, 4], BF16, name="wn_g", align_bytes=64)
 
-        def regroup_wp():
-            src = wp_raw[:].rearrange("p t e -> p e t")
-            if WP_ON_GPSIMD:
-                for h in range(2):
-                    nc.gpsimd.tensor_scalar(
-                        out=wp_g[:, 256 * h : 256 * h + 256, :], in0=src[:, 256 * h : 256 * h + 256, :],
-                        scalar1=1.0, scalar2=0.0, op0=ALU.mult, op1=ALU.add,
-                    )
-            else:
-                nc.vector.tensor_copy(
-                    out=wp_g[:].rearrange("p (c i) t -> p c t i", i=4), in_=wp_raw[:].rearrange("p t (c i) -> p c t i", i=4)
-                )
-
-        def quantise_wp():
+        def prepare_wp():
+            nc.vector.tensor_copy(
+                out=wp_g[:].rearrange("p (c i) t -> p c t i", i=4), in_=wp_raw[:].rearrange("p t (c i) -> p c t i", i=4)
+            )
             nc.vector.tensor_scalar_mul(out=wn_g[:], in0=wp_g[:], scalar1=-1.0)
             nc.vector.quantize_mx(out=wp_c[:].bitcast(FP8X4), scales=wp_s[:], in_=wp_g[:].rearrange("p e t -> p (e t)"))
             nc.vector.quantize_mx(out=wn_c[:].bitcast(FP8X4), scales=wn_s[:], in_=wn_g[:].rearrange("p e t -> p (e t)"))
@@ -117,42 +100,38 @@ def tile_qkvorthoposnegpromptg_pb_t_kernel(tc, pos_o, neg_o, Wo, bo, Wp, bp, out
         st = {}
 
         def transposes(j):
-            n = SIZES[j]
-            cols = 2 * n * P
-            xg = work.tile([P, 4 * cols], BF16, name="xg", align_bytes=64)
+            xg = work.tile([P, 4 * COLS], BF16, name="xg", align_bytes=64)
             xg_w = xg[:].bitcast(F32).rearrange("p (c u) -> p c u", u=2)
-            tiles = [(s, i) for s in range(2) for i in range(n)]
-            for b in range(cols // 256):
-                xt = ps_s.tile([P, 2, 256], F32, name="xt", tag="sx")
+            for b in range(2):
+                xt = ps_s.tile([P, 2, 2 * P], F32, name="xt", tag="sx")
                 for v in range(2):
-                    s, i = tiles[2 * b + v]
-                    words = xin[(s, j)][:, i, :].bitcast(F32)
+                    words = xin[(b, j)][:, v, :].bitcast(F32)
                     for u in range(2):
                         nc.tensor.transpose(xt[:, u, P * v : P * v + P], words[:, P * u : P * u + P], ident[:])
-                nc.scalar.copy(out=xg_w[:, 256 * b : 256 * b + 256, :], in_=xt[:].rearrange("p u c -> p c u"))
+                nc.scalar.copy(out=xg_w[:, 2 * P * b : 2 * P * b + 2 * P, :], in_=xt[:].rearrange("p u c -> p c u"))
             st[("xg", j)] = xg
-            xc = work.tile([P, cols], U32, name="xc", align_bytes=64)
-            xsc = work.tile([P, cols], U8, name="xsc", align_bytes=64)
+            xc = work.tile([P, COLS], U32, name="xc", align_bytes=64)
+            xsc = work.tile([P, COLS], U8, name="xsc", align_bytes=64)
             st[("xc", j)] = (xc, xsc)
 
-        def quant_half(j, src, dst, h):
-            w = SIZES[j] * P
+        def quantise(j, src, dst, parts):
+            w = COLS // parts
             codes, scales = st[(dst, j)]
-            nc.vector.quantize_mx(
-                out=codes[:, w * h : w * h + w].bitcast(FP8X4),
-                scales=scales[:, w * h : w * h + w],
-                in_=st[(src, j)][:, 4 * w * h : 4 * w * h + 4 * w],
-            )
+            for h in range(parts):
+                nc.vector.quantize_mx(
+                    out=codes[:, w * h : w * h + w].bitcast(FP8X4),
+                    scales=scales[:, w * h : w * h + w],
+                    in_=st[(src, j)][:, 4 * w * h : 4 * w * h + 4 * w],
+                )
 
         def hidden(j, blocks):
-            cols = 2 * SIZES[j] * P
             xc, xsc = st[("xc", j)]
             if blocks[0] == 0:
-                hb_new = work.tile([P, 4, cols], BF16, name="hb")
+                hb_new = work.tile([P, 4, COLS], BF16, name="hb")
                 st[("hb", j)] = hb_new
             hb = st[("hb", j)]
             for t in blocks:
-                hp = ps_s.tile([P, cols], F32, name="hp", tag="sx")
+                hp = ps_s.tile([P, COLS], F32, name="hp", tag="sx")
                 nc.tensor.matmul_mx(
                     out=hp[:],
                     lhsT=wo_c[:, P * t : P * t + P].bitcast(FP8X4),
@@ -162,24 +141,18 @@ def tile_qkvorthoposnegpromptg_pb_t_kernel(tc, pos_o, neg_o, Wo, bo, Wp, bp, out
                     start=True,
                     stop=True,
                 )
-                nc.scalar.activation(out=hb[:, t, :], in_=hp[:], func=ACT.Identity, bias=bo_f[:, t : t + 1], scale=1.0)
+                nc.scalar.activation(out=hb[:, t, :], in_=hp[:], func=ACT.Identity, bias=bo_raw[:, t : t + 1], scale=1.0)
 
         def regroup(j):
-            w = SIZES[j] * P
             hb = st[("hb", j)]
-            hg = work.tile([P, 8 * w], BF16, name="hg", align_bytes=64, bufs=HG_BUFS)
-            hg3 = hg[:].rearrange("p (c t) -> p c t", t=4)
-            if HEAD_V_R and j == 0:
-                nc.vector.tensor_copy(
-                    out=hg[:].rearrange("p (c i t) -> p c t i", i=4, t=4), in_=hb[:].rearrange("p t (c i) -> p c t i", i=4)
-                )
-            else:
-                nc.gpsimd.tensor_scalar(
-                    out=hg3, in0=hb[:].rearrange("p t c -> p c t"), scalar1=1.0, scalar2=0.0, op0=ALU.mult, op1=ALU.add
-                )
+            hg = work.tile([P, 4 * COLS], BF16, name="hg", align_bytes=64, bufs=1)
+            nc.gpsimd.tensor_scalar(
+                out=hg[:].rearrange("p (c t) -> p c t", t=4), in0=hb[:].rearrange("p t c -> p c t"),
+                scalar1=1.0, scalar2=0.0, op0=ALU.mult, op1=ALU.add,
+            )
             st[("hg", j)] = hg
-            hc = work.tile([P, 2 * w], U32, name="hc", align_bytes=64)
-            hs = work.tile([P, 2 * w], U8, name="hs", align_bytes=64)
+            hc = work.tile([P, COLS], U32, name="hc", align_bytes=64)
+            hs = work.tile([P, COLS], U8, name="hs", align_bytes=64)
             st[("hc", j)] = (hc, hs)
 
         def mx2(out, j, m, w_c, w_s, start, stop):
@@ -196,99 +169,84 @@ def tile_qkvorthoposnegpromptg_pb_t_kernel(tc, pos_o, neg_o, Wo, bo, Wp, bp, out
 
         def second_pos(j):
             tiles = []
-            for i in range(SIZES[j]):
+            for i in range(N):
                 a = ps_v.tile([P, D], F32, name="a")
                 mx2(a[:], j, i, wp_c, wp_s, True, True)
                 tiles.append(a)
             st[("a", j)] = tiles
 
         def second_diff(j, i):
-            d = ps_v.tile([P, D], F32, name="d", bufs=D_BUFS)
-            mx2(d[:], j, SIZES[j] + i, wp_c, wp_s, True, False)
-            mx2(d[:], j, i, wn_c, wn_s, False, True)
+            d = ps_v.tile([P, D], F32, name="d")
+            mx2(d[:], j, i, wp_c, wp_s, True, False)
+            mx2(d[:], j, N + i, wn_c, wn_s, False, True)
             st[("d", j, i)] = d
 
         def sums(j):
-            n = SIZES[j]
             a = st[("a", j)]
-            d = [st[("d", j, i)] for i in range(n)]
-            po = outp.tile([P, n, D], F32, name="po")
-            xx = small.tile([P, n], F32, name="xx")
-            ss = small.tile([P, n], F32, name="ss")
-            nden = small.tile([P, n], F32, name="nden")
-            for i in range(n):
-                nc.vector.tensor_tensor(out=po[:, i, :], in0=a[i][:], in1=beta[:], op=ALU.add)
-            for i in range(n):
-                sq = work.tile([P, D], BF16, name="sq")
-                nc.scalar.activation(out=sq[:], in_=po[:, i, :], func=ACT.Square, accum_out=xx[:, i : i + 1])
-            if NDEN_ON_SCALAR:
-                nc.scalar.activation(out=nden[:], in_=xx[:], func=ACT.Copy, bias=-EPS, scale=-1.0)
-            nc.sync.dma_start(out=outs[0][:, first[j] : first[j] + n, :], in_=po[:])
-            for i in range(n):
+            d = [st[("d", j, i)] for i in range(N)]
+            po = pos[j % PO_BUFS]
+            den = small.tile([P, N], F32, name="den")
+            ss = small.tile([P, N], F32, name="ss")
+            for i in range(N):
+                nc.vector.tensor_tensor(out=po[:, i, 0:D], in0=a[i][:], in1=bp_raw[:], op=ALU.add)
+            for i in range(N):
+                sq = work.tile([P, D + 1], BF16, name="sq")
+                nc.scalar.activation(out=sq[:], in_=po[:, i, 0 : D + 1], func=ACT.Square, accum_out=den[:, i : i + 1])
+            nc.sync.dma_start(out=outs[0][:, N * j : N * j + N, :], in_=po[:, :, 0:D])
+            for i in range(N):
                 pr = work.tile([P, D], BF16, name="pr")
                 nc.vector.scalar_tensor_tensor(
-                    out=pr[:], in0=d[i][:], scalar=1.0, in1=po[:, i, :], op0=ALU.mult, op1=ALU.mult,
+                    out=pr[:], in0=d[i][:], scalar=1.0, in1=po[:, i, 0:D], op0=ALU.mult, op1=ALU.mult,
                     accum_out=ss[:, i : i + 1],
                 )
-            st[("e", j)] = (po, xx, ss, nden)
+            st[("e", j)] = (po, den, ss)
 
         def project(j):
-            n = SIZES[j]
             po = st[("e", j)][0]
             g = st[("g", j)]
-            d = [st[("d", j, i)] for i in range(n)]
-            ng = outp.tile([P, n, D], F32, name="ng")
-            for i in range(n):
+            ng = outp.tile([P, N, D], F32, name="ng")
+            for i in range(N):
                 nc.vector.scalar_tensor_tensor(
-                    out=ng[:, i, :], in0=po[:, i, :], scalar=g[:, i : i + 1], in1=d[i][:], op0=ALU.mult, op1=ALU.add
+                    out=ng[:, i, :], in0=po[:, i, 0:D], scalar=g[:, i : i + 1], in1=st[("d", j, i)][:], op0=ALU.mult, op1=ALU.subtract
                 )
-                if j == nstep - 1:
-                    nc.sync.dma_start(out=outs[1][:, first[j] + i : first[j] + i + 1, :], in_=ng[:, i : i + 1, :])
-            if j < nstep - 1:
-                nc.sync.dma_start(out=outs[1][:, first[j] : first[j] + n, :], in_=ng[:])
+                if j == NSTEP - 1:
+                    nc.sync.dma_start(out=outs[1][:, N * j + i : N * j + i + 1, :], in_=ng[:, i : i + 1, :])
+            if j < NSTEP - 1:
+                nc.sync.dma_start(out=outs[1][:, N * j : N * j + N, :], in_=ng[:])
 
         def ok(j):
-            return 0 <= j < nstep
+            return 0 <= j < NSTEP
 
         prepare_wo()
-        for j in range(-4, nstep):
+        for j in range(-4, NSTEP):
             if ok(j):
                 sums(j)
             if ok(j + 2):
                 hidden(j + 2, (2, 3))
             if ok(j):
-                po, xx, ss, nden = st[("e", j)]
-                nrec = small.tile([P, SIZES[j]], F32, name="nrec")
-                nc.vector.reciprocal(out=nrec[:], in_=nden[:])
-            if ok(j + 1):
-                quant_half(j + 1, "hg", "hc", 0)
+                po, den, ss = st[("e", j)]
+                rec = small.tile([P, N], F32, name="rec")
+                nc.vector.reciprocal(out=rec[:], in_=den[:])
             if ok(j + 3):
-                quant_half(j + 3, "xg", "xc", 0)
-                quant_half(j + 3, "xg", "xc", 1)
+                quantise(j + 3, "xg", "xc", 1 if j >= 0 else 2)
             if ok(j):
-                g = small.tile([P, SIZES[j]], F32, name="g")
-                nc.vector.scalar_tensor_tensor(out=g[:], in0=ss[:], scalar=EPS, in1=nrec[:], op0=ALU.subtract, op1=ALU.mult)
+                g = small.tile([P, N], F32, name="g")
+                nc.vector.scalar_tensor_tensor(out=g[:], in0=ss[:], scalar=EPS, in1=rec[:], op0=ALU.add, op1=ALU.mult)
                 st[("g", j)] = g
             if ok(j + 1):
-                quant_half(j + 1, "hg", "hc", 1)
+                quantise(j + 1, "hg", "hc", 1)
             if ok(j + 2):
                 regroup(j + 2)
-            if j == -1:
-                nc.vector.tensor_copy(out=beta[:], in_=bp_raw[:])
-            if j == WP_AT:
-                regroup_wp()
-                quantise_wp()
+            if j == -2:
+                prepare_wp()
             if ok(j + 4):
                 transposes(j + 4)
-            if ok(j + 1):
-                second_pos(j + 1)
-                if D_BUFS == 3:
-                    second_diff(j + 1, 0)
             if ok(j + 3):
                 hidden(j + 3, (0, 1))
+            if ok(j + 1):
+                second_pos(j + 1)
             if ok(j):
                 project(j)
             if ok(j + 1):
-                if D_BUFS == 2:
-                    second_diff(j + 1, 0)
+                second_diff(j + 1, 0)
                 second_diff(j + 1, 1)

@@ -18,11 +18,15 @@ NT = ROWS // P
 N = 2
 NSTEP = NT // N
 COLS = 2 * N * P
+HALF = COLS // 2
 EPS = 1e-8
 ROOT_EPS = 1e-4
 PITCH = D + 16
 PO_BUFS = 3
 FLOPS = 2 * 2 * (2 * ROWS) * D * D
+
+HV = {0: (1, 3)}
+XV = {}
 
 
 def tile_qkvorthoposnegpromptg_pb_t_kernel(tc, pos_o, neg_o, Wo, bo, Wp, bp, out_0, out_1):
@@ -36,8 +40,7 @@ def tile_qkvorthoposnegpromptg_pb_t_kernel(tc, pos_o, neg_o, Wo, bo, Wp, bp, out
         work = ctx.enter_context(tc.tile_pool(name="work", bufs=2))
         outp = ctx.enter_context(tc.tile_pool(name="outp", bufs=3))
         small = ctx.enter_context(tc.tile_pool(name="small", bufs=3))
-        ps_s = ctx.enter_context(tc.psum_pool(name="ps_s", bufs=4))
-        ps_v = ctx.enter_context(tc.psum_pool(name="ps_v", bufs=2))
+        psum = ctx.enter_context(tc.psum_pool(name="psum", bufs=2))
         ctx.enter_context(tc.manual_schedule())
 
         ident = const.tile([P, P], F32, name="ident")
@@ -77,38 +80,49 @@ def tile_qkvorthoposnegpromptg_pb_t_kernel(tc, pos_o, neg_o, Wo, bo, Wp, bp, out
         wo_g = const.tile([P, 4, P, 4], BF16, name="wo_g", align_bytes=64)
         wo_c = const.tile([P, D], U32, name="wo_c", align_bytes=64)
         wo_s = const.tile([P, D], U8, name="wo_s", align_bytes=64)
-
-        def prepare_wo():
-            nc.vector.tensor_copy(out=wo_g[:], in_=wo_raw[:].rearrange("q t (m b) -> q b m t", b=4))
-            nc.vector.quantize_mx(out=wo_c[:].bitcast(FP8X4), scales=wo_s[:], in_=wo_g[:].rearrange("q b m t -> q (b m t)"))
-
+        wp_g = const.tile([P, D, 4], BF16, name="wp_g", align_bytes=64)
         wp_c = const.tile([P, D], U32, name="wp_c", align_bytes=64)
         wp_s = const.tile([P, D], U8, name="wp_s", align_bytes=64)
-        wn_c = const.tile([P, D], U32, name="wn_c", align_bytes=64)
-        wn_s = const.tile([P, D], U8, name="wn_s", align_bytes=64)
-        wp_g = const.tile([P, D, 4], BF16, name="wp_g", align_bytes=64)
-        wn_g = const.tile([P, D, 4], BF16, name="wn_g", align_bytes=64)
+
+        def prepare_wo():
+            src = wo_raw[:].rearrange("q t (m b) -> q b m t", b=4)
+            nc.vector.tensor_copy(out=wo_g[:, 0:2], in_=src[:, 0:2])
+            nc.scalar.copy(out=wo_g[:, 2:4], in_=src[:, 2:4])
+            for h in range(2):
+                cols = slice(2 * P * h, 2 * P * h + 2 * P)
+                nc.vector.quantize_mx(
+                    out=wo_c[:, cols].bitcast(FP8X4), scales=wo_s[:, cols],
+                    in_=wo_g[:, 2 * h : 2 * h + 2].rearrange("q b m t -> q (b m t)"),
+                )
 
         def prepare_wp():
             nc.vector.tensor_copy(
                 out=wp_g[:].rearrange("p (c i) t -> p c t i", i=4), in_=wp_raw[:].rearrange("p t (c i) -> p c t i", i=4)
             )
-            nc.vector.tensor_scalar_mul(out=wn_g[:], in0=wp_g[:], scalar1=-1.0)
             nc.vector.quantize_mx(out=wp_c[:].bitcast(FP8X4), scales=wp_s[:], in_=wp_g[:].rearrange("p e t -> p (e t)"))
-            nc.vector.quantize_mx(out=wn_c[:].bitcast(FP8X4), scales=wn_s[:], in_=wn_g[:].rearrange("p e t -> p (e t)"))
 
         st = {}
 
         def transposes(j):
-            xg = work.tile([P, 4 * COLS], BF16, name="xg", align_bytes=64)
-            xg_w = xg[:].bitcast(F32).rearrange("p (c u) -> p c u", u=2)
+            banks = []
             for b in range(2):
-                xt = ps_s.tile([P, 2, 2 * P], F32, name="xt", tag="sx")
+                xt = psum.tile([P, 2, 2 * P], F32, name="xt")
                 for v in range(2):
                     words = xin[(b, j)][:, v, :].bitcast(F32)
                     for u in range(2):
                         nc.tensor.transpose(xt[:, u, P * v : P * v + P], words[:, P * u : P * u + P], ident[:])
-                nc.scalar.copy(out=xg_w[:, 2 * P * b : 2 * P * b + 2 * P, :], in_=xt[:].rearrange("p u c -> p c u"))
+                banks.append(xt)
+            st[("xt", j)] = banks
+
+        def take_x(j):
+            xg = work.tile([P, 4 * COLS], BF16, name="xg", align_bytes=64)
+            words = xg[:].bitcast(F32).rearrange("p (c u) -> p c u", u=2)
+            for b in range(2):
+                dst, src = words[:, HALF * b : HALF * b + HALF, :], st[("xt", j)][b][:].rearrange("p u c -> p c u")
+                if b in XV.get(j, ()):
+                    nc.vector.tensor_copy(out=dst, in_=src)
+                else:
+                    nc.scalar.copy(out=dst, in_=src)
             st[("xg", j)] = xg
             xc = work.tile([P, COLS], U32, name="xc", align_bytes=64)
             xsc = work.tile([P, COLS], U8, name="xsc", align_bytes=64)
@@ -131,7 +145,7 @@ def tile_qkvorthoposnegpromptg_pb_t_kernel(tc, pos_o, neg_o, Wo, bo, Wp, bp, out
                 st[("hb", j)] = hb_new
             hb = st[("hb", j)]
             for t in blocks:
-                hp = ps_s.tile([P, COLS], F32, name="hp", tag="sx")
+                hp = psum.tile([P, COLS], F32, name="hp")
                 nc.tensor.matmul_mx(
                     out=hp[:],
                     lhsT=wo_c[:, P * t : P * t + P].bitcast(FP8X4),
@@ -141,54 +155,64 @@ def tile_qkvorthoposnegpromptg_pb_t_kernel(tc, pos_o, neg_o, Wo, bo, Wp, bp, out
                     start=True,
                     stop=True,
                 )
-                nc.scalar.activation(out=hb[:, t, :], in_=hp[:], func=ACT.Identity, bias=bo_raw[:, t : t + 1], scale=1.0)
+                if t in HV.get(j, ()):
+                    nc.vector.tensor_scalar(out=hb[:, t, :], in0=hp[:], scalar1=bo_raw[:, t : t + 1], scalar2=None, op0=ALU.add)
+                else:
+                    nc.scalar.activation(out=hb[:, t, :], in_=hp[:], func=ACT.Identity, bias=bo_raw[:, t : t + 1], scale=1.0)
 
         def regroup(j):
             hb = st[("hb", j)]
             hg = work.tile([P, 4 * COLS], BF16, name="hg", align_bytes=64, bufs=1)
-            nc.gpsimd.tensor_scalar(
-                out=hg[:].rearrange("p (c t) -> p c t", t=4), in0=hb[:].rearrange("p t c -> p c t"),
-                scalar1=1.0, scalar2=0.0, op0=ALU.mult, op1=ALU.add,
-            )
+            for s, sign in enumerate((1.0, -1.0)):
+                cols = slice(HALF * s, HALF * s + HALF)
+                words = hg[:, 4 * HALF * s : 4 * HALF * s + 4 * HALF]
+                if j == 0:
+                    nc.vector.tensor_scalar_mul(
+                        out=words.rearrange("p (c i t) -> p c t i", i=4, t=4),
+                        in0=hb[:, :, cols].rearrange("p t (c i) -> p c t i", i=4),
+                        scalar1=sign,
+                    )
+                else:
+                    nc.gpsimd.tensor_scalar(
+                        out=words.rearrange("p (c t) -> p c t", t=4), in0=hb[:, :, cols].rearrange("p t c -> p c t"),
+                        scalar1=sign, scalar2=0.0, op0=ALU.mult, op1=ALU.add,
+                    )
             st[("hg", j)] = hg
             hc = work.tile([P, COLS], U32, name="hc", align_bytes=64)
             hs = work.tile([P, COLS], U8, name="hs", align_bytes=64)
             st[("hc", j)] = (hc, hs)
 
-        def mx2(out, j, m, w_c, w_s, start, stop):
+        def second(out, j, m, start, stop):
             hc, hs = st[("hc", j)]
             nc.tensor.matmul_mx(
                 out=out,
                 lhsT=hc[:, P * m : P * m + P].bitcast(FP8X4),
                 lhsT_scale=hs[:, P * m : P * m + P],
-                rhs=w_c[:].bitcast(FP8X4),
-                rhs_scale=w_s[:],
+                rhs=wp_c[:].bitcast(FP8X4),
+                rhs_scale=wp_s[:],
                 start=start,
                 stop=stop,
             )
 
         def second_pos(j):
-            tiles = []
             for i in range(N):
-                a = ps_v.tile([P, D], F32, name="a")
-                mx2(a[:], j, i, wp_c, wp_s, True, True)
-                tiles.append(a)
-            st[("a", j)] = tiles
+                a = psum.tile([P, D], F32, name="a")
+                second(a[:], j, i, True, True)
+                st[("a", j, i)] = a
 
-        def second_diff(j, i):
-            d = ps_v.tile([P, D], F32, name="d")
-            mx2(d[:], j, i, wp_c, wp_s, True, False)
-            mx2(d[:], j, N + i, wn_c, wn_s, False, True)
-            st[("d", j, i)] = d
+        def second_diff(j):
+            for i in range(N):
+                d = psum.tile([P, D], F32, name="d")
+                second(d[:], j, i, True, False)
+                second(d[:], j, N + i, False, True)
+                st[("d", j, i)] = d
 
         def sums(j):
-            a = st[("a", j)]
-            d = [st[("d", j, i)] for i in range(N)]
             po = pos[j % PO_BUFS]
             den = small.tile([P, N], F32, name="den")
             ss = small.tile([P, N], F32, name="ss")
             for i in range(N):
-                nc.vector.tensor_tensor(out=po[:, i, 0:D], in0=a[i][:], in1=bp_raw[:], op=ALU.add)
+                nc.vector.tensor_tensor(out=po[:, i, 0:D], in0=st[("a", j, i)][:], in1=bp_raw[:], op=ALU.add)
             for i in range(N):
                 sq = work.tile([P, D + 1], BF16, name="sq")
                 nc.scalar.activation(out=sq[:], in_=po[:, i, 0 : D + 1], func=ACT.Square, accum_out=den[:, i : i + 1])
@@ -196,7 +220,7 @@ def tile_qkvorthoposnegpromptg_pb_t_kernel(tc, pos_o, neg_o, Wo, bo, Wp, bp, out
             for i in range(N):
                 pr = work.tile([P, D], BF16, name="pr")
                 nc.vector.scalar_tensor_tensor(
-                    out=pr[:], in0=d[i][:], scalar=1.0, in1=po[:, i, 0:D], op0=ALU.mult, op1=ALU.mult,
+                    out=pr[:], in0=st[("d", j, i)][:], scalar=1.0, in1=po[:, i, 0:D], op0=ALU.mult, op1=ALU.mult,
                     accum_out=ss[:, i : i + 1],
                 )
             st[("e", j)] = (po, den, ss)
@@ -205,12 +229,14 @@ def tile_qkvorthoposnegpromptg_pb_t_kernel(tc, pos_o, neg_o, Wo, bo, Wp, bp, out
             po = st[("e", j)][0]
             g = st[("g", j)]
             ng = outp.tile([P, N, D], F32, name="ng")
-            for i in range(N):
+            pieces = [(0, 0, D), (1, 0, D // 2), (1, D // 2, D)] if j == NSTEP - 1 else [(i, 0, D) for i in range(N)]
+            for i, lo, hi in pieces:
                 nc.vector.scalar_tensor_tensor(
-                    out=ng[:, i, :], in0=po[:, i, 0:D], scalar=g[:, i : i + 1], in1=st[("d", j, i)][:], op0=ALU.mult, op1=ALU.subtract
+                    out=ng[:, i, lo:hi], in0=po[:, i, lo:hi], scalar=g[:, i : i + 1], in1=st[("d", j, i)][:, lo:hi],
+                    op0=ALU.mult, op1=ALU.subtract,
                 )
                 if j == NSTEP - 1:
-                    nc.sync.dma_start(out=outs[1][:, N * j + i : N * j + i + 1, :], in_=ng[:, i : i + 1, :])
+                    nc.sync.dma_start(out=outs[1][:, N * j + i, lo:hi], in_=ng[:, i, lo:hi])
             if j < NSTEP - 1:
                 nc.sync.dma_start(out=outs[1][:, N * j : N * j + N, :], in_=ng[:])
 
@@ -221,32 +247,35 @@ def tile_qkvorthoposnegpromptg_pb_t_kernel(tc, pos_o, neg_o, Wo, bo, Wp, bp, out
         for j in range(-4, NSTEP):
             if ok(j):
                 sums(j)
+                if ok(j + 4):
+                    transposes(j + 4)
             if ok(j + 2):
                 hidden(j + 2, (2, 3))
+            if ok(j + 4):
+                if j < 0:
+                    transposes(j + 4)
+                take_x(j + 4)
             if ok(j):
                 po, den, ss = st[("e", j)]
                 rec = small.tile([P, N], F32, name="rec")
                 nc.vector.reciprocal(out=rec[:], in_=den[:])
-            if ok(j + 3):
-                quantise(j + 3, "xg", "xc", 1 if j >= 0 else 2)
+            if ok(j + 1):
+                quantise(j + 1, "hg", "hc", 1)
             if ok(j):
                 g = small.tile([P, N], F32, name="g")
                 nc.vector.scalar_tensor_tensor(out=g[:], in0=ss[:], scalar=EPS, in1=rec[:], op0=ALU.add, op1=ALU.mult)
                 st[("g", j)] = g
-            if ok(j + 1):
-                quantise(j + 1, "hg", "hc", 1)
+            if ok(j + 3):
+                quantise(j + 3, "xg", "xc", 1 if j >= 0 else 2)
             if ok(j + 2):
                 regroup(j + 2)
             if j == -2:
                 prepare_wp()
-            if ok(j + 4):
-                transposes(j + 4)
-            if ok(j + 3):
-                hidden(j + 3, (0, 1))
             if ok(j + 1):
                 second_pos(j + 1)
+            if ok(j + 3):
+                hidden(j + 3, (0, 1))
             if ok(j):
                 project(j)
             if ok(j + 1):
-                second_diff(j + 1, 0)
-                second_diff(j + 1, 1)
+                second_diff(j + 1)

@@ -25,8 +25,8 @@ PITCH = D + 16
 PO_BUFS = 3
 FLOPS = 2 * 2 * (2 * ROWS) * D * D
 
-HV = {0: (1, 3)}
-XV = {}
+HIDDEN_ON_VECTOR = {0: (1, 3)}
+X_ON_VECTOR = {2: (1,), 3: (1,)}
 
 
 def tile_qkvorthoposnegpromptg_pb_t_kernel(tc, pos_o, neg_o, Wo, bo, Wp, bp, out_0, out_1):
@@ -43,6 +43,9 @@ def tile_qkvorthoposnegpromptg_pb_t_kernel(tc, pos_o, neg_o, Wo, bo, Wp, bp, out
         psum = ctx.enter_context(tc.psum_pool(name="psum", bufs=2))
         ctx.enter_context(tc.manual_schedule())
 
+        table = const.tile([P, 1], F32, name="table")
+        nc.vector.memset(table[:], 0.0)
+        nc.scalar.activation(out=table[:], in_=table[:], func=ACT.Square)
         ident = const.tile([P, P], F32, name="ident")
         make_identity(nc, ident[:])
         bo_raw = const.tile([P, 4], BF16, name="bo_raw")
@@ -85,9 +88,7 @@ def tile_qkvorthoposnegpromptg_pb_t_kernel(tc, pos_o, neg_o, Wo, bo, Wp, bp, out
         wp_s = const.tile([P, D], U8, name="wp_s", align_bytes=64)
 
         def prepare_wo():
-            src = wo_raw[:].rearrange("q t (m b) -> q b m t", b=4)
-            nc.vector.tensor_copy(out=wo_g[:, 0:2], in_=src[:, 0:2])
-            nc.scalar.copy(out=wo_g[:, 2:4], in_=src[:, 2:4])
+            nc.vector.tensor_copy(out=wo_g[:], in_=wo_raw[:].rearrange("q t (m b) -> q b m t", b=4))
             for h in range(2):
                 cols = slice(2 * P * h, 2 * P * h + 2 * P)
                 nc.vector.quantize_mx(
@@ -95,10 +96,12 @@ def tile_qkvorthoposnegpromptg_pb_t_kernel(tc, pos_o, neg_o, Wo, bo, Wp, bp, out
                     in_=wo_g[:, 2 * h : 2 * h + 2].rearrange("q b m t -> q (b m t)"),
                 )
 
-        def prepare_wp():
+        def regroup_wp():
             nc.vector.tensor_copy(
                 out=wp_g[:].rearrange("p (c i) t -> p c t i", i=4), in_=wp_raw[:].rearrange("p t (c i) -> p c t i", i=4)
             )
+
+        def quantise_wp():
             nc.vector.quantize_mx(out=wp_c[:].bitcast(FP8X4), scales=wp_s[:], in_=wp_g[:].rearrange("p e t -> p (e t)"))
 
         st = {}
@@ -119,7 +122,7 @@ def tile_qkvorthoposnegpromptg_pb_t_kernel(tc, pos_o, neg_o, Wo, bo, Wp, bp, out
             words = xg[:].bitcast(F32).rearrange("p (c u) -> p c u", u=2)
             for b in range(2):
                 dst, src = words[:, HALF * b : HALF * b + HALF, :], st[("xt", j)][b][:].rearrange("p u c -> p c u")
-                if b in XV.get(j, ()):
+                if b in X_ON_VECTOR.get(j, ()):
                     nc.vector.tensor_copy(out=dst, in_=src)
                 else:
                     nc.scalar.copy(out=dst, in_=src)
@@ -145,7 +148,7 @@ def tile_qkvorthoposnegpromptg_pb_t_kernel(tc, pos_o, neg_o, Wo, bo, Wp, bp, out
                 st[("hb", j)] = hb_new
             hb = st[("hb", j)]
             for t in blocks:
-                hp = psum.tile([P, COLS], F32, name="hp")
+                hp = psum.tile([P, COLS], F32, name="hp", tag="d" if j == 0 and t >= 2 else "hp")
                 nc.tensor.matmul_mx(
                     out=hp[:],
                     lhsT=wo_c[:, P * t : P * t + P].bitcast(FP8X4),
@@ -155,7 +158,7 @@ def tile_qkvorthoposnegpromptg_pb_t_kernel(tc, pos_o, neg_o, Wo, bo, Wp, bp, out
                     start=True,
                     stop=True,
                 )
-                if t in HV.get(j, ()):
+                if t in HIDDEN_ON_VECTOR.get(j, ()):
                     nc.vector.tensor_scalar(out=hb[:, t, :], in0=hp[:], scalar1=bo_raw[:, t : t + 1], scalar2=None, op0=ALU.add)
                 else:
                     nc.scalar.activation(out=hb[:, t, :], in_=hp[:], func=ACT.Identity, bias=bo_raw[:, t : t + 1], scale=1.0)
@@ -244,38 +247,51 @@ def tile_qkvorthoposnegpromptg_pb_t_kernel(tc, pos_o, neg_o, Wo, bo, Wp, bp, out
             return 0 <= j < NSTEP
 
         prepare_wo()
-        for j in range(-4, NSTEP):
-            if ok(j):
-                sums(j)
-                if ok(j + 4):
-                    transposes(j + 4)
+        transposes(0)
+        take_x(0)
+        quantise(0, "xg", "xc", 2)
+        transposes(1)
+        take_x(1)
+        quantise(1, "xg", "xc", 2)
+        hidden(0, (0, 1, 2, 3))
+        regroup_wp()
+        regroup(0)
+        transposes(2)
+        take_x(2)
+        hidden(1, (0, 1, 2, 3))
+        quantise(2, "xg", "xc", 2)
+        quantise(0, "hg", "hc", 2)
+        quantise_wp()
+        transposes(3)
+        take_x(3)
+        hidden(2, (0, 1))
+        second_pos(0)
+        second_diff(0)
+        regroup(1)
+        for j in range(NSTEP):
+            sums(j)
+            if ok(j + 4):
+                transposes(j + 4)
             if ok(j + 2):
                 hidden(j + 2, (2, 3))
             if ok(j + 4):
-                if j < 0:
-                    transposes(j + 4)
                 take_x(j + 4)
-            if ok(j):
-                po, den, ss = st[("e", j)]
-                rec = small.tile([P, N], F32, name="rec")
-                nc.vector.reciprocal(out=rec[:], in_=den[:])
+            po, den, ss = st[("e", j)]
+            rec = small.tile([P, N], F32, name="rec")
+            nc.vector.reciprocal(out=rec[:], in_=den[:])
             if ok(j + 1):
                 quantise(j + 1, "hg", "hc", 1)
-            if ok(j):
-                g = small.tile([P, N], F32, name="g")
-                nc.vector.scalar_tensor_tensor(out=g[:], in0=ss[:], scalar=EPS, in1=rec[:], op0=ALU.add, op1=ALU.mult)
-                st[("g", j)] = g
+            g = small.tile([P, N], F32, name="g")
+            nc.vector.scalar_tensor_tensor(out=g[:], in0=ss[:], scalar=EPS, in1=rec[:], op0=ALU.add, op1=ALU.mult)
+            st[("g", j)] = g
             if ok(j + 3):
-                quantise(j + 3, "xg", "xc", 1 if j >= 0 else 2)
+                quantise(j + 3, "xg", "xc", 1)
             if ok(j + 2):
                 regroup(j + 2)
-            if j == -2:
-                prepare_wp()
             if ok(j + 1):
                 second_pos(j + 1)
             if ok(j + 3):
                 hidden(j + 3, (0, 1))
-            if ok(j):
-                project(j)
+            project(j)
             if ok(j + 1):
                 second_diff(j + 1)

@@ -25,8 +25,8 @@ PITCH = D + 16
 PO_BUFS = 3
 FLOPS = 2 * 2 * (2 * ROWS) * D * D
 
-HIDDEN_ON_VECTOR = {0: (1, 3)}
-X_ON_VECTOR = {2: (1,), 3: (1,)}
+X_ON_VECTOR = {2: (1,)}
+PROJECT_AWAY = (NSTEP - 2, 1)
 
 
 def tile_qkvorthoposnegpromptg_pb_t_kernel(tc, pos_o, neg_o, Wo, bo, Wp, bp, out_0, out_1):
@@ -158,10 +158,7 @@ def tile_qkvorthoposnegpromptg_pb_t_kernel(tc, pos_o, neg_o, Wo, bo, Wp, bp, out
                     start=True,
                     stop=True,
                 )
-                if t in HIDDEN_ON_VECTOR.get(j, ()):
-                    nc.vector.tensor_scalar(out=hb[:, t, :], in0=hp[:], scalar1=bo_raw[:, t : t + 1], scalar2=None, op0=ALU.add)
-                else:
-                    nc.scalar.activation(out=hb[:, t, :], in_=hp[:], func=ACT.Identity, bias=bo_raw[:, t : t + 1], scale=1.0)
+                nc.scalar.activation(out=hb[:, t, :], in_=hp[:], func=ACT.Identity, bias=bo_raw[:, t : t + 1], scale=1.0)
 
         def regroup(j):
             hb = st[("hb", j)]
@@ -234,6 +231,13 @@ def tile_qkvorthoposnegpromptg_pb_t_kernel(tc, pos_o, neg_o, Wo, bo, Wp, bp, out
             ng = outp.tile([P, N, D], F32, name="ng")
             pieces = [(0, 0, D), (1, 0, D // 2), (1, D // 2, D)] if j == NSTEP - 1 else [(i, 0, D) for i in range(N)]
             for i, lo, hi in pieces:
+                if (j, i) == PROJECT_AWAY:
+                    dc = work.tile([P, D], F32, name="dc")
+                    nc.scalar.copy(out=dc[:], in_=st[("d", j, i)][:])
+                    gp = work.tile([P, D], F32, name="gp")
+                    nc.scalar.activation(out=gp[:], in_=po[:, i, 0:D], func=ACT.Copy, scale=g[:, i : i + 1])
+                    nc.gpsimd.tensor_tensor(out=ng[:, i, :], in0=gp[:], in1=dc[:], op=ALU.subtract)
+                    continue
                 nc.vector.scalar_tensor_tensor(
                     out=ng[:, i, lo:hi], in0=po[:, i, lo:hi], scalar=g[:, i : i + 1], in1=st[("d", j, i)][:, lo:hi],
                     op0=ALU.mult, op1=ALU.subtract,
@@ -255,13 +259,13 @@ def tile_qkvorthoposnegpromptg_pb_t_kernel(tc, pos_o, neg_o, Wo, bo, Wp, bp, out
         quantise(1, "xg", "xc", 2)
         hidden(0, (0, 1, 2, 3))
         regroup_wp()
+        quantise_wp()
         regroup(0)
         transposes(2)
         take_x(2)
         hidden(1, (0, 1, 2, 3))
         quantise(2, "xg", "xc", 2)
         quantise(0, "hg", "hc", 2)
-        quantise_wp()
         transposes(3)
         take_x(3)
         hidden(2, (0, 1))

@@ -131,15 +131,15 @@ def tile_qkvorthoposnegpromptg_pb_t_kernel(tc, pos_o, neg_o, Wo, bo, Wp, bp, out
             xsc = work.tile([P, COLS], U8, name="xsc", align_bytes=64)
             st[("xc", j)] = (xc, xsc)
 
-        def quantise(j, src, dst, parts):
-            w = COLS // parts
+        def quantise(j, src, dst, lo=0, hi=COLS):
             codes, scales = st[(dst, j)]
-            for h in range(parts):
-                nc.vector.quantize_mx(
-                    out=codes[:, w * h : w * h + w].bitcast(FP8X4),
-                    scales=scales[:, w * h : w * h + w],
-                    in_=st[(src, j)][:, 4 * w * h : 4 * w * h + 4 * w],
-                )
+            nc.vector.quantize_mx(
+                out=codes[:, lo:hi].bitcast(FP8X4), scales=scales[:, lo:hi], in_=st[(src, j)][:, 4 * lo : 4 * hi]
+            )
+
+        def quantise_halves(j, src, dst):
+            quantise(j, src, dst, 0, HALF)
+            quantise(j, src, dst, HALF, COLS)
 
         def hidden(j, blocks):
             xc, xsc = st[("xc", j)]
@@ -253,10 +253,10 @@ def tile_qkvorthoposnegpromptg_pb_t_kernel(tc, pos_o, neg_o, Wo, bo, Wp, bp, out
         prepare_wo()
         transposes(0)
         take_x(0)
-        quantise(0, "xg", "xc", 2)
+        quantise_halves(0, "xg", "xc")
         transposes(1)
         take_x(1)
-        quantise(1, "xg", "xc", 2)
+        quantise_halves(1, "xg", "xc")
         hidden(0, (0, 1, 2, 3))
         regroup_wp()
         quantise_wp()
@@ -264,8 +264,8 @@ def tile_qkvorthoposnegpromptg_pb_t_kernel(tc, pos_o, neg_o, Wo, bo, Wp, bp, out
         transposes(2)
         take_x(2)
         hidden(1, (0, 1, 2, 3))
-        quantise(2, "xg", "xc", 2)
-        quantise(0, "hg", "hc", 2)
+        quantise_halves(2, "xg", "xc")
+        quantise_halves(0, "hg", "hc")
         transposes(3)
         take_x(3)
         hidden(2, (0, 1))
@@ -283,13 +283,16 @@ def tile_qkvorthoposnegpromptg_pb_t_kernel(tc, pos_o, neg_o, Wo, bo, Wp, bp, out
             po, den, ss = st[("e", j)]
             rec = small.tile([P, N], F32, name="rec")
             nc.vector.reciprocal(out=rec[:], in_=den[:])
+            whole = ok(j + 3)
             if ok(j + 1):
-                quantise(j + 1, "hg", "hc", 1)
+                quantise(j + 1, "hg", "hc", 0, COLS if whole else HALF)
             g = small.tile([P, N], F32, name="g")
             nc.vector.scalar_tensor_tensor(out=g[:], in0=ss[:], scalar=EPS, in1=rec[:], op0=ALU.add, op1=ALU.mult)
             st[("g", j)] = g
-            if ok(j + 3):
-                quantise(j + 3, "xg", "xc", 1)
+            if whole:
+                quantise(j + 3, "xg", "xc")
+            elif ok(j + 1):
+                quantise(j + 1, "hg", "hc", HALF, COLS)
             if ok(j + 2):
                 regroup(j + 2)
             if ok(j + 1):

@@ -283,22 +283,21 @@ def tile_qkvorthoposnegpromptg_pb_t_kernel(tc, pos_o, neg_o, Wo, bo, Wp, bp, out
             po, den, ss = st[("e", j)]
             rec = small.tile([P, N], F32, name="rec")
             nc.vector.reciprocal(out=rec[:], in_=den[:])
-            whole = ok(j + 3)
-            if ok(j + 1):
-                quantise(j + 1, "hg", "hc", 0, COLS if whole else HALF)
+            if ok(j + 3):
+                quantise(j + 3, "xg", "xc")
+            elif ok(j + 1):
+                quantise(j + 1, "hg", "hc", 0, HALF)
             g = small.tile([P, N], F32, name="g")
             nc.vector.scalar_tensor_tensor(out=g[:], in0=ss[:], scalar=EPS, in1=rec[:], op0=ALU.add, op1=ALU.mult)
             st[("g", j)] = g
-            if whole:
-                quantise(j + 3, "xg", "xc")
-            elif ok(j + 1):
-                quantise(j + 1, "hg", "hc", HALF, COLS)
+            if ok(j + 1):
+                quantise(j + 1, "hg", "hc", 0 if ok(j + 3) else HALF, COLS)
             if ok(j + 2):
                 regroup(j + 2)
-            if ok(j + 1):
-                second_pos(j + 1)
             if ok(j + 3):
                 hidden(j + 3, (0, 1))
+            if ok(j + 1):
+                second_pos(j + 1)
             project(j)
             if ok(j + 1):
                 second_diff(j + 1)

@@ -174,7 +174,8 @@ def tile_qkvorthoposnegpromptg_pb_t_kernel(tc, pos_o, neg_o, Wo, bo, Wp, bp, out
                     )
                 else:
                     nc.gpsimd.tensor_scalar(
-                        out=words.rearrange("p (c t) -> p c t", t=4), in0=hb[:, :, cols].rearrange("p t c -> p c t"),
+                        out=words.rearrange("p (c i t) -> p c t i", i=4, t=4),
+                        in0=hb[:, :, cols].rearrange("p t (c i) -> p c t i", i=4),
                         scalar1=sign, scalar2=0.0, op0=ALU.mult, op1=ALU.add,
                     )
             st[("hg", j)] = hg

from contextlib import ExitStack

import concourse.mybir as mybir
from concourse.masks import make_identity

F32 = mybir.dt.float32
BF16 = mybir.dt.bfloat16
U32 = mybir.dt.uint32
U8 = mybir.dt.uint8
FP8X4 = mybir.dt.float8_e4m3fn_x4
ALU = mybir.AluOpType
ACT = mybir.ActivationFunctionType

P = 128
D = 512
ROWS = 4096
NT = ROWS // P
N = 2
NSTEP = NT // N
COLS = 2 * N * P
HALF = COLS // 2
EPS = 1e-8
ROOT_EPS = 1e-4
PITCH = D + 16
PO_BUFS = 3
FLOPS = 2 * 2 * (2 * ROWS) * D * D

X_ON_VECTOR = {2: (1,)}
PROJECT_AWAY = (NSTEP - 2, 1)


def tile_qkvorthoposnegpromptg_pb_t_kernel(tc, pos_o, neg_o, Wo, bo, Wp, bp, out_0, out_1):
    nc = tc.nc
    xs = [a.flatten_outer_dims().rearrange("(p n) k -> p n k", n=NT) for a in (pos_o, neg_o)]
    outs = [a.flatten_outer_dims().rearrange("(p n) e -> p n e", n=NT) for a in (out_0, out_1)]

    with ExitStack() as ctx:
        const = ctx.enter_context(tc.tile_pool(name="const", bufs=1))
        xpool = ctx.enter_context(tc.tile_pool(name="xpool", bufs=1))
        work = ctx.enter_context(tc.tile_pool(name="work", bufs=2))
        outp = ctx.enter_context(tc.tile_pool(name="outp", bufs=3))
        small = ctx.enter_context(tc.tile_pool(name="small", bufs=3))
        psum = ctx.enter_context(tc.psum_pool(name="psum", bufs=2))
        ctx.enter_context(tc.manual_schedule())

        table = const.tile([P, 1], F32, name="table")
        nc.vector.memset(table[:], 0.0)
        nc.scalar.activation(out=table[:], in_=table[:], func=ACT.Square)
        ident = const.tile([P, P], F32, name="ident")
        make_identity(nc, ident[:])
        bo_raw = const.tile([P, 4], BF16, name="bo_raw")
        nc.sync.dma_start(out=bo_raw[:], in_=bo.rearrange("(p t) -> p t", t=4))
        bp_raw = const.tile([P, D], BF16, name="bp_raw")
        pos = []
        for i in range(PO_BUFS):
            t = const.tile([P, N, PITCH], F32, name="po_%d" % i)
            nc.gpsimd.memset(t[:, :, D : D + 1], ROOT_EPS)
            pos.append(t)

        xin = {}

        def load_x(j):
            for s in range(2):
                t = xpool.tile([P, N, D], BF16, name="xin_%d_%d" % (s, j))
                nc.sync.dma_start(out=t[:], in_=xs[s][:, N * j : N * j + N, :])
                xin[(s, j)] = t

        wo_raw = const.tile([P, 4, D], BF16, name="wo_raw")
        for u in range(2):
            nc.sync.dma_start(
                out=wo_raw[:, 2 * u : 2 * u + 2, :],
                in_=Wo[256 * u : 256 * u + 256, :].rearrange("(q e) c -> q e c", e=2),
            )
        load_x(0)
        load_x(1)
        wp_raw = const.tile([P, 4, D], BF16, name="wp_raw")
        nc.sync.dma_start(out=wp_raw[:], in_=Wp.rearrange("(p t) e -> p t e", t=4))
        for j in range(2, NSTEP):
            load_x(j)
            if j == 3:
                nc.sync.dma_start(out=bp_raw[:], in_=bp.partition_broadcast(P))

        wo_g = const.tile([P, 4, P, 4], BF16, name="wo_g", align_bytes=64)
        wo_c = const.tile([P, D], U32, name="wo_c", align_bytes=64)
        wo_s = const.tile([P, D], U8, name="wo_s", align_bytes=64)
        wp_g = const.tile([P, D, 4], BF16, name="wp_g", align_bytes=64)
        wp_c = const.tile([P, D], U32, name="wp_c", align_bytes=64)
        wp_s = const.tile([P, D], U8, name="wp_s", align_bytes=64)

        def prepare_wo():
            nc.vector.tensor_copy(out=wo_g[:], in_=wo_raw[:].rearrange("q t (m b) -> q b m t", b=4))
            for h in range(2):
                cols = slice(2 * P * h, 2 * P * h + 2 * P)
                nc.vector.quantize_mx(
                    out=wo_c[:, cols].bitcast(FP8X4), scales=wo_s[:, cols],
                    in_=wo_g[:, 2 * h : 2 * h + 2].rearrange("q b m t -> q (b m t)"),
                )

        def regroup_wp():
            nc.vector.tensor_copy(
                out=wp_g[:].rearrange("p (c i) t -> p c t i", i=4), in_=wp_raw[:].rearrange("p t (c i) -> p c t i", i=4)
            )

        def quantise_wp():
            nc.vector.quantize_mx(out=wp_c[:].bitcast(FP8X4), scales=wp_s[:], in_=wp_g[:].rearrange("p e t -> p (e t)"))

        st = {}

        def transposes(j):
            banks = []
            for b in range(2):
                xt = psum.tile([P, 2, 2 * P], F32, name="xt")
                for v in range(2):
                    words = xin[(b, j)][:, v, :].bitcast(F32)
                    for u in range(2):
                        nc.tensor.transpose(xt[:, u, P * v : P * v + P], words[:, P * u : P * u + P], ident[:])
                banks.append(xt)
            st[("xt", j)] = banks

        def take_x(j):
            xg = work.tile([P, 4 * COLS], BF16, name="xg", align_bytes=64)
            words = xg[:].bitcast(F32).rearrange("p (c u) -> p c u", u=2)
            for b in range(2):
                dst, src = words[:, HALF * b : HALF * b + HALF, :], st[("xt", j)][b][:].rearrange("p u c -> p c u")
                if b in X_ON_VECTOR.get(j, ()):
                    nc.vector.tensor_copy(out=dst, in_=src)
                else:
                    nc.scalar.copy(out=dst, in_=src)
            st[("xg", j)] = xg
            xc = work.tile([P, COLS], U32, name="xc", align_bytes=64)
            xsc = work.tile([P, COLS], U8, name="xsc", align_bytes=64)
            st[("xc", j)] = (xc, xsc)

        def quantise(j, src, dst, lo=0, hi=COLS):
            codes, scales = st[(dst, j)]
            nc.vector.quantize_mx(
                out=codes[:, lo:hi].bitcast(FP8X4), scales=scales[:, lo:hi], in_=st[(src, j)][:, 4 * lo : 4 * hi]
            )

        def quantise_halves(j, src, dst):
            quantise(j, src, dst, 0, HALF)
            quantise(j, src, dst, HALF, COLS)

        def hidden(j, blocks):
            xc, xsc = st[("xc", j)]
            if blocks[0] == 0:
                hb_new = work.tile([P, 4, COLS], BF16, name="hb")
                st[("hb", j)] = hb_new
            hb = st[("hb", j)]
            for t in blocks:
                hp = psum.tile([P, COLS], F32, name="hp", tag="d" if j == 0 and t >= 2 else "hp")
                nc.tensor.matmul_mx(
                    out=hp[:],
                    lhsT=wo_c[:, P * t : P * t + P].bitcast(FP8X4),
                    lhsT_scale=wo_s[:, P * t : P * t + P],
                    rhs=xc[:].bitcast(FP8X4),
                    rhs_scale=xsc[:],
                    start=True,
                    stop=True,
                )
                nc.scalar.activation(out=hb[:, t, :], in_=hp[:], func=ACT.Identity, bias=bo_raw[:, t : t + 1], scale=1.0)

        def regroup(j):
            hb = st[("hb", j)]
            hg = work.tile([P, 4 * COLS], BF16, name="hg", align_bytes=64, bufs=1)
            for s, sign in enumerate((1.0, -1.0)):
                cols = slice(HALF * s, HALF * s + HALF)
                words = hg[:, 4 * HALF * s : 4 * HALF * s + 4 * HALF]
                if j == 0:
                    nc.vector.tensor_scalar_mul(
                        out=words.rearrange("p (c i t) -> p c t i", i=4, t=4),
                        in0=hb[:, :, cols].rearrange("p t (c i) -> p c t i", i=4),
                        scalar1=sign,
                    )
                else:
                    nc.gpsimd.tensor_scalar(
                        out=words.rearrange("p (c i t) -> p c t i", i=4, t=4),
                        in0=hb[:, :, cols].rearrange("p t (c i) -> p c t i", i=4),
                        scalar1=sign, scalar2=0.0, op0=ALU.mult, op1=ALU.add,
                    )
            st[("hg", j)] = hg
            hc = work.tile([P, COLS], U32, name="hc", align_bytes=64)
            hs = work.tile([P, COLS], U8, name="hs", align_bytes=64)
            st[("hc", j)] = (hc, hs)

        def second(out, j, m, start, stop):
            hc, hs = st[("hc", j)]
            nc.tensor.matmul_mx(
                out=out,
                lhsT=hc[:, P * m : P * m + P].bitcast(FP8X4),
                lhsT_scale=hs[:, P * m : P * m + P],
                rhs=wp_c[:].bitcast(FP8X4),
                rhs_scale=wp_s[:],
                start=start,
                stop=stop,
            )

        def second_pos(j):
            for i in range(N):
                a = psum.tile([P, D], F32, name="a")
                second(a[:], j, i, True, True)
                st[("a", j, i)] = a

        def second_diff(j):
            for i in range(N):
                d = psum.tile([P, D], F32, name="d")
                second(d[:], j, i, True, False)
                second(d[:], j, N + i, False, True)
                st[("d", j, i)] = d

        def sums(j):
            po = pos[j % PO_BUFS]
            den = small.tile([P, N], F32, name="den")
            ss = small.tile([P, N], F32, name="ss")
            for i in range(N):
                nc.vector.tensor_tensor(out=po[:, i, 0:D], in0=st[("a", j, i)][:], in1=bp_raw[:], op=ALU.add)
            for i in range(N):
                sq = work.tile([P, D + 1], BF16, name="sq")
                nc.scalar.activation(out=sq[:], in_=po[:, i, 0 : D + 1], func=ACT.Square, accum_out=den[:, i : i + 1])
            nc.sync.dma_start(out=outs[0][:, N * j : N * j + N, :], in_=po[:, :, 0:D])
            for i in range(N):
                pr = work.tile([P, D], BF16, name="pr")
                nc.vector.scalar_tensor_tensor(
                    out=pr[:], in0=st[("d", j, i)][:], scalar=1.0, in1=po[:, i, 0:D], op0=ALU.mult, op1=ALU.mult,
                    accum_out=ss[:, i : i + 1],
                )
            st[("e", j)] = (po, den, ss)

        def project(j):
            po = st[("e", j)][0]
            g = st[("g", j)]
            ng = outp.tile([P, N, D], F32, name="ng")
            pieces = [(0, 0, D), (1, 0, D // 2), (1, D // 2, D)] if j == NSTEP - 1 else [(i, 0, D) for i in range(N)]
            for i, lo, hi in pieces:
                if (j, i) == PROJECT_AWAY:
                    dc = work.tile([P, D], F32, name="dc")
                    nc.scalar.copy(out=dc[:], in_=st[("d", j, i)][:])
                    gp = work.tile([P, D], F32, name="gp")
                    nc.scalar.activation(out=gp[:], in_=po[:, i, 0:D], func=ACT.Copy, scale=g[:, i : i + 1])
                    nc.gpsimd.tensor_tensor(out=ng[:, i, :], in0=gp[:], in1=dc[:], op=ALU.subtract)
                    continue
                nc.vector.scalar_tensor_tensor(
                    out=ng[:, i, lo:hi], in0=po[:, i, lo:hi], scalar=g[:, i : i + 1], in1=st[("d", j, i)][:, lo:hi],
                    op0=ALU.mult, op1=ALU.subtract,
                )
                if j == NSTEP - 1:
                    nc.sync.dma_start(out=outs[1][:, N * j + i, lo:hi], in_=ng[:, i, lo:hi])
            if j < NSTEP - 1:
                nc.sync.dma_start(out=outs[1][:, N * j : N * j + N, :], in_=ng[:])

        def ok(j):
            return 0 <= j < NSTEP

        prepare_wo()
        transposes(0)
        take_x(0)
        quantise_halves(0, "xg", "xc")
        transposes(1)
        take_x(1)
        quantise_halves(1, "xg", "xc")
        hidden(0, (0, 1, 2, 3))
        regroup_wp()
        quantise_wp()
        regroup(0)
        transposes(2)
        take_x(2)
        hidden(1, (0, 1, 2, 3))
        quantise_halves(2, "xg", "xc")
        quantise_halves(0, "hg", "hc")
        transposes(3)
        take_x(3)
        hidden(2, (0, 1))
        second_pos(0)
        second_diff(0)
        regroup(1)
        for j in range(NSTEP):
            sums(j)
            if ok(j + 4):
                transposes(j + 4)
            if ok(j + 2):
                hidden(j + 2, (2, 3))
            if ok(j + 4):
                take_x(j + 4)
            po, den, ss = st[("e", j)]
            rec = small.tile([P, N], F32, name="rec")
            nc.vector.reciprocal(out=rec[:], in_=den[:])
            if ok(j + 3):
                quantise(j + 3, "xg", "xc")
            elif ok(j + 1):
                quantise(j + 1, "hg", "hc", 0, HALF)
            g = small.tile([P, N], F32, name="g")
            nc.vector.scalar_tensor_tensor(out=g[:], in0=ss[:], scalar=EPS, in1=rec[:], op0=ALU.add, op1=ALU.mult)
            st[("g", j)] = g
            if ok(j + 1):
                quantise(j + 1, "hg", "hc", 0 if ok(j + 3) else HALF, COLS)
            if ok(j + 2):
                regroup(j + 2)
            if ok(j + 3):
                hidden(j + 3, (0, 1))
            if ok(j + 1):
                second_pos(j + 1)
            project(j)
            if ok(j + 1):
                second_diff(j + 1)
